import numpy as np
import ml_dtypes


def mxq(x, axis, fmt="e4m3"):
    dtype, down = {"e4m3": (ml_dtypes.float8_e4m3fn, 7), "e5m2": (ml_dtypes.float8_e5m2, 14)}[fmt]
    v = np.moveaxis(np.asarray(x, np.float32).astype(ml_dtypes.bfloat16).astype(np.float64), axis, -1)
    blocks = v.reshape(v.shape[:-1] + (-1, 32))
    amax = np.abs(blocks).max(-1, keepdims=True)
    byte = np.maximum(np.where(amax > 0, np.frexp(amax)[1] - 1 + 127, 0) - down, 1)
    scale = np.exp2(byte - 127.0)
    codes = (blocks / scale).astype(np.float32).astype(dtype).astype(np.float64)
    return np.moveaxis((codes * scale).reshape(v.shape), -1, axis)


WIDE = False


def mx_kscale(k):
    if not WIDE:
        return np.ones(k)
    levels = np.array([10, -10, 5, -5, 0])
    if k % 512:
        return np.exp2(np.random.permutation(np.resize(levels, k // 32))).repeat(32)
    a = np.empty((k // 512, 16))
    for p in range(k // 512):
        a[p, :8] = np.random.permutation(np.resize(levels, 8))
        for g in range(8):
            far = levels[np.abs(levels - a[p, g]) >= 10]
            a[p, g + 8] = far[np.random.randint(len(far))]
    return np.exp2(a.ravel()).repeat(32)


BF16 = ml_dtypes.bfloat16


def bf(x):
    return np.asarray(x, np.float32).astype(BF16)


def f64(x):
    return np.asarray(x).astype(np.float64)


B, L, H, E, WINDOW, QB = 1, 1024, 16, 128, 512, 512
MXB = 32


def alibi_slopes():
    return np.exp2(-8.0 * (np.arange(H) + 1.0) / H)


def setup_inputs():
    z = np.random.standard_normal((B, L, 3, H, E))
    z[:, :, 2] *= (0.5 / np.sqrt(alibi_slopes()))[:, None]
    s = mx_kscale(L)
    t = np.where((np.arange(L) // MXB) % 2 == 0, s.min(), s) / s.min()
    hs = slice(H // 2, H)
    z[:, :, 2, hs] *= t[None, :, None, None]
    z[:, :, 0, hs, 0] = np.sqrt(E) * np.log(2.0)
    z[:, :, 1, hs, 0] -= np.log2(t)[None, :, None]
    return {"qkv": bf(z)}


def reference(qkv):
    qkv = f64(qkv)
    q = qkv[:, :, 0].transpose(0, 2, 1, 3)
    k = qkv[:, :, 1].transpose(0, 2, 1, 3)
    vq = mxq(qkv[:, :, 2].transpose(0, 2, 1, 3), 2, "e4m3")
    slopes = alibi_slopes()
    outs = []
    for q0 in range(0, L, QB):
        q1 = q0 + QB
        k0 = max(0, q0 - WINDOW)
        s = q[:, :, q0:q1] @ k[:, :, k0:q1].transpose(0, 1, 3, 2) * (1.0 / E ** 0.5)
        dist = np.arange(q0, q1)[:, None] - np.arange(k0, q1)[None, :]
        s = s - slopes[None, :, None, None] * dist
        s = np.where((dist >= 0) & (dist < WINDOW), s, -np.inf)
        e = np.exp(s - s.max(-1, keepdims=True))
        outs.append((mxq(e, 3, "e4m3") @ vq[:, :, k0:q1]) / e.sum(-1, keepdims=True))
    return np.concatenate(outs, 2).transpose(0, 2, 1, 3)

@@ -1,0 +1,387 @@
+from contextlib import ExitStack
+import math
+
+import concourse.mybir as mybir
+from concourse.masks import make_identity
+
+F32 = mybir.dt.float32
+BF16 = mybir.dt.bfloat16
+U32 = mybir.dt.uint32
+U8 = mybir.dt.uint8
+FP8X4 = mybir.dt.float8_e4m3fn_x4
+ALU = mybir.AluOpType
+ACT = mybir.ActivationFunctionType
+
+P = 128
+H = 16
+L = 1024
+E = 128
+NQB = L // P
+GH = 4
+NG = NQB * H // GH
+NT = NQB * H
+SCALE = 1.0 / math.sqrt(E)
+MASKED = 1.0e30
+FLOPS = 4 * E * H * (512 * 512 + 512 * 1024)
+
+N_TP = 3
+N_E = 4
+N_X = 3
+VEC_BANKS = (1, 1, 1, 1, 2, 2, 2, 2)
+GP_BIAS_FROM = 4
+LAG_PASS, LAG_EXP, LAG_TR, LAG_COPY, LAG_Q = 1, 3, 5, 6, 8
+G_QKT, G_QKCOPY, G_BIAS, G_W, G_WPASS, G_V, G_VQ, G_MX, G_OUT = -8, -6, -6, -1, 0, 2, 4, 17, 18
+
+
+def tile_flexattention_kernel(tc, qkv, out):
+    nc = tc.nc
+    with ExitStack() as ctx:
+        ctx.enter_context(tc.manual_schedule())
+        const = ctx.enter_context(tc.tile_pool(name="const", bufs=1))
+        ld = ctx.enter_context(tc.tile_pool(name="ld", bufs=N_X))
+        qpool = ctx.enter_context(tc.tile_pool(name="qpool", bufs=4))
+        vpool = ctx.enter_context(tc.tile_pool(name="vpool", bufs=2))
+        small = ctx.enter_context(tc.tile_pool(name="small", bufs=8))
+        gsmall = ctx.enter_context(tc.tile_pool(name="gsmall", bufs=7))
+        zpool = ctx.enter_context(tc.tile_pool(name="zpool", bufs=8))
+        gpool = ctx.enter_context(tc.tile_pool(name="gpool", bufs=4))
+        cpool = ctx.enter_context(tc.tile_pool(name="cpool", bufs=12))
+        opool = ctx.enter_context(tc.tile_pool(name="opool", bufs=3))
+        ps_s = ctx.enter_context(tc.psum_pool(name="ps_s", bufs=3))
+        ps_t = ctx.enter_context(tc.psum_pool(name="ps_t", bufs=1))
+        ps_a = ctx.enter_context(tc.psum_pool(name="ps_a", bufs=2))
+
+        xs = {}
+        vraw = const.tile([P, 2, 4, H * E], BF16, name="vraw")
+        vsrc = qkv[0, :, 2].rearrange("(c p t) h e -> p c t (h e)", p=P, t=4)
+
+        def load_x(pb, pieces=1):
+            x = ld.tile([P, 2, H * E], BF16, tag="x", name="x")
+            src = qkv[0, pb * P : (pb + 1) * P, 0:2].rearrange("p w h e -> p w (h e)")
+            width = H * E // pieces
+            for i in range(pieces):
+                nc.sync.dma_start(
+                    out=x[:, :, i * width : (i + 1) * width], in_=src[:, :, i * width : (i + 1) * width]
+                )
+            xs[pb] = x
+
+        load_x(0, pieces=H // GH)
+        nc.sync.dma_start(out=vraw[:, 0], in_=vsrc[:, 0])
+        for pb in range(1, N_X):
+            load_x(pb)
+        nc.sync.dma_start(out=vraw[:, 1], in_=vsrc[:, 1])
+
+        ident_bf = const.tile([P, P], BF16, name="ident_bf")
+        make_identity(nc, ident_bf[:])
+        perm_bf = const.tile([P, P], BF16, name="perm_bf")
+        nc.vector.tensor_copy(
+            out=perm_bf[:].rearrange("p (u r w) -> p u r w", u=2, w=2),
+            in_=ident_bf[:].rearrange("p (r u w) -> p u r w", u=2, w=2),
+        )
+        dist_t = const.tile([P, 5, P], F32, name="dist_t")
+        nc.gpsimd.iota(
+            dist_t[:],
+            pattern=[[P, 5], [1, P]],
+            base=0,
+            channel_multiplier=-1,
+            allow_small_or_imprecise_dtypes=True,
+        )
+        nc.gpsimd.affine_select(
+            out=dist_t[:, 0, :], in_=dist_t[:, 0, :], pattern=[[1, P]],
+            compare_op=ALU.is_ge, fill=MASKED, base=0, channel_multiplier=-1,
+        )
+        nc.gpsimd.affine_select(
+            out=dist_t[:, 4, :], in_=dist_t[:, 4, :], pattern=[[-1, P]],
+            compare_op=ALU.is_gt, fill=MASKED, base=0, channel_multiplier=1,
+        )
+        ident_f = const.tile([P, P], F32, name="ident_f")
+        make_identity(nc, ident_f[:])
+        perm_f = const.tile([P, P], F32, name="perm_f")
+        nc.vector.tensor_copy(
+            out=perm_f[:].rearrange("p (u r w) -> p u r w", u=2, w=2),
+            in_=ident_f[:].rearrange("p (r u w) -> p u r w", u=2, w=2),
+        )
+        es = [const.tile([P, 2, 8, 64], BF16, name="e%d" % i) for i in range(N_E)]
+        for e in es:
+            nc.vector.memset(e[:], 0.0)
+        bias_t = const.tile([P, H, 5, P], F32, name="bias_t")
+        k_t = const.tile([P, H, L], BF16, name="k_t")
+        vcodes = const.tile([P, 2, H * E], U32, name="vcodes", align_bytes=64)
+        vscales = const.tile([P, 2, H * E], U8, name="vscales", align_bytes=64)
+        tps = [ps_t.tile([P, 2, 2, P], F32, name="tp%d" % i) for i in range(N_TP)]
+        counters = {"tp": 0, "e": 0}
+        st = {}
+
+        def where(n):
+            return n // H, (n % H) // GH, n % GH, n % H
+
+        def g_bias(g):
+            for h in range(GH * g, GH * g + GH):
+                sigma = 2.0 ** (-(h + 1) / 2.0) * math.sqrt(E)
+                if h >= GP_BIAS_FROM:
+                    nc.gpsimd.tensor_scalar(
+                        out=bias_t[:, h], in0=dist_t[:], scalar1=-sigma, scalar2=0.0,
+                        op0=ALU.mult, op1=ALU.add,
+                    )
+                else:
+                    nc.vector.tensor_scalar(
+                        out=bias_t[:, h], in0=dist_t[:], scalar1=-sigma, scalar2=None, op0=ALU.mult
+                    )
+
+        def g_qk_transpose(g):
+            qb, hg = g // 4, g % 4
+            qk_ps = ps_a.tile([P, 8, P], BF16, tag="a", name="qk_ps")
+            for j in range(GH):
+                h = GH * hg + j
+                nc.tensor.transpose(qk_ps[:, j, :], xs[qb][:, 0, h * E : (h + 1) * E], ident_bf[:])
+                nc.tensor.transpose(
+                    qk_ps[:, GH + j, :], xs[qb][:, 1, h * E : (h + 1) * E], perm_bf[:]
+                )
+            st["qk_ps", g] = qk_ps
+
+        def g_qk_copy(g):
+            qb, hg = g // 4, g % 4
+            qk_ps = st["qk_ps", g]
+            q_t = qpool.tile([P, GH, P], BF16, tag="q_t", name="q_t")
+            nc.scalar.copy(out=q_t[:].bitcast(F32), in_=qk_ps[:, 0:GH, :].bitcast(F32))
+            nc.scalar.copy(
+                out=k_t[:, GH * hg : GH * hg + GH, qb * P : (qb + 1) * P].bitcast(F32),
+                in_=qk_ps[:, GH : 2 * GH, :].bitcast(F32),
+            )
+            st["q_t", g] = q_t
+
+        def g_v(g):
+            c, hg = g // 16, g % 4
+            cols = slice(hg * GH * E, (hg + 1) * GH * E)
+            gv = vpool.tile([P, GH * E, 4], BF16, tag="gv", name="gv", align_bytes=64)
+            nc.vector.tensor_copy(
+                out=gv[:].rearrange("p (c i) t -> p c t i", i=4),
+                in_=vraw[:, c, :, cols].rearrange("p t (c i) -> p c t i", i=4),
+            )
+            st["gv", g] = gv
+
+        def g_v_quantise(g):
+            c, hg = g // 16, g % 4
+            cols = slice(hg * GH * E, (hg + 1) * GH * E)
+            nc.vector.quantize_mx(
+                out=vcodes[:, c, cols].bitcast(FP8X4),
+                scales=vscales[:, c, cols],
+                in_=st["gv", g][:].rearrange("p x t -> p (x t)"),
+            )
+
+        def g_window_scores(g):
+            qb, hg = g // 4, g % 4
+            wb = ps_a.tile([P, GH, P], F32, tag="a", name="wb")
+            q_t = st["q_t", g]
+            for j in range(GH):
+                h = GH * hg + j
+                nc.tensor.matmul(
+                    wb[:, j, :], lhsT=bias_t[:, h, 4, :], rhs=perm_f[:],
+                    is_transpose=True, start=True, stop=False,
+                )
+                nc.tensor.matmul(
+                    wb[:, j, :], lhsT=q_t[:, j, :], rhs=k_t[:, h, (qb - 4) * P : (qb - 3) * P],
+                    start=False, stop=True,
+                )
+            st["wb", g] = wb
+
+        def g_window_pass(g):
+            mw = gsmall.tile([P, GH], F32, tag="mw", name="mw")
+            for j in range(GH):
+                z = zpool.tile([P, 5 * P], F32, tag="z", name="z")
+                nc.vector.tensor_scalar(
+                    out=z[:, 0:P], in0=st["wb", g][:, j, :], scalar1=-SCALE, scalar2=None,
+                    op0=ALU.mult, op1=ALU.min, accum_out=mw[:, j : j + 1],
+                )
+                st["z", GH * g + j] = z
+            st["mw", g] = mw
+
+        def g_mx(g):
+            qb, hg = g // 4, g % 4
+            ob = ps_a.tile([P, GH, P], F32, tag="a", name="ob")
+            for j in range(GH):
+                h = GH * hg + j
+                fcols = slice(h * E, (h + 1) * E)
+                if qb >= 4:
+                    codes, scl = st["codes", GH * g + j]
+                    passes = [(0, 0), (1, 1)]
+                else:
+                    codes, scl = st["codes", GH * g + (j // 2) * 2 + 1]
+                    passes = [(j % 2, 0)]
+                for i, (half, c) in enumerate(passes):
+                    qcols = slice(half * P, (half + 1) * P)
+                    nc.tensor.matmul_mx(
+                        out=ob[:, j, :],
+                        lhsT=codes[:, qcols].bitcast(FP8X4),
+                        lhsT_scale=scl[:, qcols],
+                        rhs=vcodes[:, c, fcols].bitcast(FP8X4),
+                        rhs_scale=vscales[:, c, fcols],
+                        start=(i == 0),
+                        stop=(i == len(passes) - 1),
+                    )
+            st["ob", g] = ob
+
+        def g_out(g):
+            qb, hg = g // 4, g % 4
+            rinv = gsmall.tile([P, GH], F32, tag="rinv", name="rinv")
+            nc.vector.reciprocal(out=rinv[:], in_=st["rs", g][:])
+            ost = opool.tile([P, GH, P], F32, tag="ost", name="ost")
+            nc.vector.tensor_tensor(
+                out=ost[:], in0=st["ob", g][:], in1=rinv[:].unsqueeze(2).to_broadcast([P, GH, P]),
+                op=ALU.mult,
+            )
+            nc.sync.dma_start(out=out[0, qb * P : (qb + 1) * P, GH * hg : GH * hg + GH, :], in_=ost[:])
+
+        def t_scores(n):
+            qb, hg, j, h = where(n)
+            nb = min(qb + 1, 4)
+            sb = ps_s.tile([P, 4 * P], F32, tag="s", name="sb")
+            for b in range(nb):
+                nc.tensor.matmul(
+                    sb[:, b * P : (b + 1) * P], lhsT=bias_t[:, h, nb - 1 - b, :], rhs=perm_f[:],
+                    is_transpose=True, start=(b == 0), stop=False,
+                )
+            nc.tensor.matmul(
+                sb[:, 0 : nb * P], lhsT=st["q_t", n // GH][:, j, :],
+                rhs=k_t[:, h, (qb - nb + 1) * P : (qb + 1) * P], start=False, stop=True,
+            )
+            st["sb", n] = sb
+
+        def t_pass(n):
+            qb, hg, j, h = where(n)
+            nb = min(qb + 1, 4)
+            nbias = small.tile([P, 1], F32, tag="nbias", name="nbias")
+            if qb >= 4:
+                z = st["z", n]
+                first = st["mw", n // GH][:, j : j + 1]
+            else:
+                z = zpool.tile([P, 5 * P], F32, tag="z", name="z")
+                st["z", n] = z
+                first = None
+            nc.vector.tensor_scalar(
+                out=z[:, P : P + nb * P], in0=st["sb", n][:, 0 : nb * P], scalar1=-SCALE, scalar2=first,
+                op0=ALU.mult, op1=ALU.min, accum_out=nbias[:],
+            )
+            st["nbias", n] = nbias
+
+        def t_exp(n):
+            qb, hg, j, h = where(n)
+            nb = min(qb + 1, 4)
+            g = n // GH
+            if j == 0:
+                st["rs", g] = gsmall.tile([P, GH], F32, tag="rs", name="rs")
+            if qb >= 4 or j % 2 == 0:
+                e = es[counters["e"] % N_E]
+                counters["e"] += 1
+                if h < (N_E if qb >= 4 else 0):
+                    if qb == 4:
+                        nc.gpsimd.memset(e[:, :, 5:8, :], 0.0)
+                    else:
+                        nc.gpsimd.memset(e[:, :, qb - 5 : qb - 4, :], 0.0)
+                st["e_now"] = e
+            e = st["e_now"]
+            if qb >= 4:
+                lo, k0, k1 = 0, qb - 4, qb + 1
+            else:
+                lo, k0, k1 = P, 4 * (j % 2), 4 * (j % 2) + nb
+            nc.scalar.activation(
+                out=e[:, :, k0:k1, :],
+                in_=st["z", n][:, lo : P + nb * P].rearrange("p (b u w) -> p u b w", u=2, w=64),
+                func=ACT.Exp, bias=st["nbias", n][:], scale=-1.0, accum_out=st["rs", g][:, j : j + 1],
+            )
+            st["e", n] = e
+
+        def t_transpose(n):
+            qb, hg, j, h = where(n)
+            if qb >= 4 or j % 2 == 0:
+                st["bank_now"] = tps[counters["tp"] % N_TP]
+                counters["tp"] += 1
+            bank = st["bank_now"]
+            words = st["e", n][:].rearrange("p u k w -> p (u k w)").bitcast(F32)
+            for c in range(2) if qb >= 4 else (j % 2,):
+                for u in range(2):
+                    first = (2 * u + c) * P
+                    nc.tensor.transpose(bank[:, u, c, :], words[:, first : first + P], ident_f[:])
+            st["bank", n] = bank
+
+        def t_copy(n):
+            qb, hg, j, h = where(n)
+            if qb < 4 and j % 2 == 0:
+                return
+            grp = gpool.tile([P, 2, P, 4], BF16, tag="grp", name="grp", align_bytes=64)
+            dst = grp[:].rearrange("p c q t -> p (c q t)").bitcast(F32).rearrange("p (c q u) -> p c q u", c=2, u=2)
+            src = st["bank", n][:].rearrange("p u c q -> p c q u")
+            units, u = (8, h // 2) if qb < 4 else (16, h)
+            if (u + 1) * VEC_BANKS[qb] // units > u * VEC_BANKS[qb] // units:
+                nc.vector.tensor_copy(out=dst, in_=src)
+            else:
+                nc.scalar.copy(out=dst, in_=src)
+            st["grp", n] = grp
+
+        def t_quantise(n):
+            qb, hg, j, h = where(n)
+            if qb < 4 and j % 2 == 0:
+                return
+            codes = cpool.tile([P, 2 * P], U32, tag="codes", name="codes", align_bytes=64)
+            scl = cpool.tile([P, 2 * P], U8, tag="scl", name="scl", align_bytes=64)
+            nc.vector.quantize_mx(
+                out=codes[:].bitcast(FP8X4), scales=scl[:],
+                in_=st["grp", n][:].rearrange("p g q t -> p (g q t)"),
+            )
+            st["codes", n] = (codes, scl)
+
+        def tile_at(s, lag):
+            return s - lag if 0 <= s - lag < NT else None
+
+        def group_at(s, off, lo=0, hi=NG):
+            g, r = divmod(s - off, GH)
+            return g if r == 0 and lo <= g < hi else None
+
+        for s in range(G_QKT, NT + G_OUT):
+            n = tile_at(s, 0)
+            if n is not None:
+                t_scores(n)
+            n = tile_at(s, LAG_TR)
+            if n is not None:
+                t_transpose(n)
+            g = group_at(s, G_QKT)
+            if g is not None:
+                g_qk_transpose(g)
+            g = group_at(s, G_W, lo=16)
+            if g is not None:
+                g_window_scores(g)
+            g = group_at(s, G_MX)
+            if g is not None:
+                g_mx(g)
+            g = group_at(s, G_BIAS, hi=4)
+            if g is not None:
+                g_bias(g)
+            g = group_at(s, G_QKCOPY)
+            if g is not None:
+                g_qk_copy(g)
+            g = group_at(s, G_WPASS, lo=16)
+            if g is not None:
+                g_window_pass(g)
+            n = tile_at(s, LAG_PASS)
+            if n is not None:
+                t_pass(n)
+            n = tile_at(s, LAG_EXP)
+            if n is not None:
+                t_exp(n)
+            n = tile_at(s, LAG_COPY)
+            if n is not None:
+                t_copy(n)
+            n = tile_at(s, LAG_Q)
+            if n is not None:
+                t_quantise(n)
+            g = group_at(s, G_V)
+            if g is not None and g % 16 < 4:
+                g_v(g)
+            g = group_at(s, G_VQ)
+            if g is not None and g % 16 < 4:
+                g_v_quantise(g)
+            g = group_at(s, G_OUT)
+            if g is not None:
+                g_out(g)
+            if s % H == 6 and N_X <= s // H + N_X < NQB:
+                load_x(s // H + N_X)

@@ -6,6 +6,7 @@ from concourse.masks import make_identity
 
 F32 = mybir.dt.float32
 BF16 = mybir.dt.bfloat16
+I32 = mybir.dt.int32
 U32 = mybir.dt.uint32
 U8 = mybir.dt.uint8
 FP8X4 = mybir.dt.float8_e4m3fn_x4
@@ -18,19 +19,24 @@ L = 1024
 E = 128
 NQB = L // P
 GH = 4
-NG = NQB * H // GH
-NT = NQB * H
+NHG = H // GH
+GT = 4
+NG = 2 * H
+NT = GT * NG
+HGT = NT // NHG
 SCALE = 1.0 / math.sqrt(E)
 MASKED = 1.0e30
 FLOPS = 4 * E * H * (512 * 512 + 512 * 1024)
 
 N_TP = 3
-N_E = 4
-N_X = 3
-VEC_BANKS = (1, 1, 1, 1, 2, 2, 2, 2)
-GP_BIAS_FROM = 4
+N_E = 3
 LAG_PASS, LAG_EXP, LAG_TR, LAG_COPY, LAG_Q = 1, 3, 5, 6, 8
-G_QKT, G_QKCOPY, G_BIAS, G_W, G_WPASS, G_V, G_VQ, G_MX, G_OUT = -8, -6, -6, -1, 0, 2, 4, 17, 18
+G_QKT, G_QKCOPY, G_W, G_WPASS, G_MX, G_OUT = -8, -6, -1, 0, 17, 18
+V_STEPS = ((15, 17), (19, 21))
+V_STEPS_FIRST = ((2, 3), (5, 6))
+BIAS_AHEAD = 12
+
+HALF0_PLACE = ((1, 3), (0, 0), (1, 0), (2, 0))
 
 
 def tile_flexattention_kernel(tc, qkv, out):
@@ -38,38 +44,48 @@ def tile_flexattention_kernel(tc, qkv, out):
     with ExitStack() as ctx:
         ctx.enter_context(tc.manual_schedule())
         const = ctx.enter_context(tc.tile_pool(name="const", bufs=1))
-        ld = ctx.enter_context(tc.tile_pool(name="ld", bufs=N_X))
+        ld = ctx.enter_context(tc.tile_pool(name="ld", bufs=2))
+        bpool = ctx.enter_context(tc.tile_pool(name="bpool", bufs=4))
+        kpool = ctx.enter_context(tc.tile_pool(name="kpool", bufs=4))
         qpool = ctx.enter_context(tc.tile_pool(name="qpool", bufs=4))
         vpool = ctx.enter_context(tc.tile_pool(name="vpool", bufs=2))
         small = ctx.enter_context(tc.tile_pool(name="small", bufs=8))
-        gsmall = ctx.enter_context(tc.tile_pool(name="gsmall", bufs=7))
+        gsmall = ctx.enter_context(tc.tile_pool(name="gsmall", bufs=8))
         zpool = ctx.enter_context(tc.tile_pool(name="zpool", bufs=8))
         gpool = ctx.enter_context(tc.tile_pool(name="gpool", bufs=4))
         cpool = ctx.enter_context(tc.tile_pool(name="cpool", bufs=12))
         opool = ctx.enter_context(tc.tile_pool(name="opool", bufs=3))
         ps_s = ctx.enter_context(tc.psum_pool(name="ps_s", bufs=3))
-        ps_t = ctx.enter_context(tc.psum_pool(name="ps_t", bufs=1))
+        ps_t = ctx.enter_context(tc.psum_pool(name="ps_t", bufs=N_TP))
         ps_a = ctx.enter_context(tc.psum_pool(name="ps_a", bufs=2))
 
-        xs = {}
-        vraw = const.tile([P, 2, 4, H * E], BF16, name="vraw")
+        st = {}
+
+        qksrc = qkv[0].rearrange("(b p) w h e -> p b w (h e)", p=P)
         vsrc = qkv[0, :, 2].rearrange("(c p t) h e -> p c t (h e)", p=P, t=4)
 
-        def load_x(pb, pieces=1):
-            x = ld.tile([P, 2, H * E], BF16, tag="x", name="x")
-            src = qkv[0, pb * P : (pb + 1) * P, 0:2].rearrange("p w h e -> p w (h e)")
-            width = H * E // pieces
-            for i in range(pieces):
+        def load_qk(hg, half):
+            if half == 0:
+                st["x", hg] = ld.tile([P, NQB, 2, GH * E], BF16, tag="x", name="x")
+            for b in range(4 * half, 4 * half + 4):
                 nc.sync.dma_start(
-                    out=x[:, :, i * width : (i + 1) * width], in_=src[:, :, i * width : (i + 1) * width]
+                    out=st["x", hg][:, b], in_=qksrc[:, b, 0:2, hg * GH * E : (hg + 1) * GH * E]
                 )
-            xs[pb] = x
 
-        load_x(0, pieces=H // GH)
-        nc.sync.dma_start(out=vraw[:, 0], in_=vsrc[:, 0])
-        for pb in range(1, N_X):
-            load_x(pb)
-        nc.sync.dma_start(out=vraw[:, 1], in_=vsrc[:, 1])
+        def load_v(hg, c):
+            if c == 0:
+                st["vraw", hg] = ld.tile([P, 2, 4, GH * E], BF16, tag="vraw", name="vraw")
+            nc.sync.dma_start(
+                out=st["vraw", hg][:, c], in_=vsrc[:, c, :, hg * GH * E : (hg + 1) * GH * E]
+            )
+
+        def load(hg):
+            for half in range(2):
+                load_qk(hg, half)
+                load_v(hg, half)
+
+        load(0)
+        load(1)
 
         ident_bf = const.tile([P, P], BF16, name="ident_bf")
         make_identity(nc, ident_bf[:])
@@ -101,159 +117,190 @@ def tile_flexattention_kernel(tc, qkv, out):
             out=perm_f[:].rearrange("p (u r w) -> p u r w", u=2, w=2),
             in_=ident_f[:].rearrange("p (r u w) -> p u r w", u=2, w=2),
         )
-        es = [const.tile([P, 2, 8, 64], BF16, name="e%d" % i) for i in range(N_E)]
-        for e in es:
-            nc.vector.memset(e[:], 0.0)
-        bias_t = const.tile([P, H, 5, P], F32, name="bias_t")
-        k_t = const.tile([P, H, L], BF16, name="k_t")
-        vcodes = const.tile([P, 2, H * E], U32, name="vcodes", align_bytes=64)
-        vscales = const.tile([P, 2, H * E], U8, name="vscales", align_bytes=64)
-        tps = [ps_t.tile([P, 2, 2, P], F32, name="tp%d" % i) for i in range(N_TP)]
-        counters = {"tp": 0, "e": 0}
-        st = {}
+        es = (
+            [const.tile([P, 2, 12, 64], BF16, name="ea%d" % i) for i in range(N_E)],
+            [const.tile([P, 2, 20, 64], BF16, name="eb%d" % i) for i in range(N_E)],
+        )
+        for e in es[0]:
+            nc.vector.memset(e[:, :, 2:4, :], 0.0)
+        VARIANTS = {
+            ("hi", 1): (0, 32, 128), ("hi", 2): (0, 64, 128), ("hi", 3): (0, 96, 128),
+            ("lo", 0): (1, 0, 32), ("lo", 1): (1, 0, 64), ("lo", 2): (1, 0, 96),
+            ("first", 2): (0, 0, 96), ("moved", 0): (0, 0, 32),
+        }
+        vvar = [
+            {key: const.tile([P, GH * E], U32, name="v%s%d%d" % (key[0], key[1], i), align_bytes=64) for key in VARIANTS}
+            for i in range(2)
+        ]
+        vmscales = [const.tile([P, GH * E], U8, name="vms%d" % i, align_bytes=64) for i in range(2)]
+        for i in range(2):
+            for key in VARIANTS:
+                nc.gpsimd.memset(vvar[i][key][:], 0)
+            nc.gpsimd.memset(vmscales[i][:].bitcast(U32), 0)
 
         def where(n):
-            return n // H, (n % H) // GH, n % GH, n % H
+            g, j = divmod(n, GT)
+            h, half = divmod(g, 2)
+            return g, h, half, j, (4 if half else j + 1)
 
-        def g_bias(g):
-            for h in range(GH * g, GH * g + GH):
-                sigma = 2.0 ** (-(h + 1) / 2.0) * math.sqrt(E)
-                if h >= GP_BIAS_FROM:
-                    nc.gpsimd.tensor_scalar(
-                        out=bias_t[:, h], in0=dist_t[:], scalar1=-sigma, scalar2=0.0,
-                        op0=ALU.mult, op1=ALU.add,
-                    )
-                else:
-                    nc.vector.tensor_scalar(
-                        out=bias_t[:, h], in0=dist_t[:], scalar1=-sigma, scalar2=None, op0=ALU.mult
-                    )
-
-        def g_qk_transpose(g):
-            qb, hg = g // 4, g % 4
-            qk_ps = ps_a.tile([P, 8, P], BF16, tag="a", name="qk_ps")
-            for j in range(GH):
-                h = GH * hg + j
-                nc.tensor.transpose(qk_ps[:, j, :], xs[qb][:, 0, h * E : (h + 1) * E], ident_bf[:])
-                nc.tensor.transpose(
-                    qk_ps[:, GH + j, :], xs[qb][:, 1, h * E : (h + 1) * E], perm_bf[:]
-                )
-            st["qk_ps", g] = qk_ps
-
-        def g_qk_copy(g):
-            qb, hg = g // 4, g % 4
-            qk_ps = st["qk_ps", g]
-            q_t = qpool.tile([P, GH, P], BF16, tag="q_t", name="q_t")
-            nc.scalar.copy(out=q_t[:].bitcast(F32), in_=qk_ps[:, 0:GH, :].bitcast(F32))
-            nc.scalar.copy(
-                out=k_t[:, GH * hg : GH * hg + GH, qb * P : (qb + 1) * P].bitcast(F32),
-                in_=qk_ps[:, GH : 2 * GH, :].bitcast(F32),
-            )
-            st["q_t", g] = q_t
-
-        def g_v(g):
-            c, hg = g // 16, g % 4
-            cols = slice(hg * GH * E, (hg + 1) * GH * E)
+        def v_copy(hg, c):
             gv = vpool.tile([P, GH * E, 4], BF16, tag="gv", name="gv", align_bytes=64)
             nc.vector.tensor_copy(
                 out=gv[:].rearrange("p (c i) t -> p c t i", i=4),
-                in_=vraw[:, c, :, cols].rearrange("p t (c i) -> p c t i", i=4),
+                in_=st["vraw", hg][:, c].rearrange("p t (c i) -> p c t i", i=4),
             )
-            st["gv", g] = gv
+            st["gv", hg, c] = gv
 
-        def g_v_quantise(g):
-            c, hg = g // 16, g % 4
-            cols = slice(hg * GH * E, (hg + 1) * GH * E)
+        def v_quantise(hg, c):
+            codes = vpool.tile([P, GH * E], U32, tag="vcodes%d" % c, name="vcodes", align_bytes=64)
+            scl = vpool.tile([P, GH * E], U8, tag="vscales%d" % c, name="vscales", align_bytes=64)
             nc.vector.quantize_mx(
-                out=vcodes[:, c, cols].bitcast(FP8X4),
-                scales=vscales[:, c, cols],
-                in_=st["gv", g][:].rearrange("p x t -> p (x t)"),
+                out=codes[:].bitcast(FP8X4), scales=scl[:],
+                in_=st["gv", hg, c][:].rearrange("p x t -> p (x t)"),
             )
+            st["v", hg, c] = (codes, scl)
+            for key, (half, p0, p1) in VARIANTS.items():
+                if half == c:
+                    q0, q1 = (96, 128) if key[0] == "moved" else (p0, p1)
+                    nc.sync.dma_start(
+                        out=vvar[hg % 2][key][q0:q1, :].bitcast(I32), in_=codes[p0:p1, :].bitcast(I32)
+                    )
+            if c == 0:
+                nc.sync.dma_start(out=vmscales[hg % 2][96:100, :].bitcast(I32), in_=scl[0:4, :].bitcast(I32))
+
+        def h_bias(h):
+            sigma = 2.0 ** (-(h + 1) / 2.0) * math.sqrt(E)
+            bias_t = bpool.tile([P, 5, P], F32, tag="bias", name="bias_t")
+            if h > 1:
+                nc.gpsimd.tensor_scalar(
+                    out=bias_t[:], in0=dist_t[:], scalar1=-sigma, scalar2=0.0, op0=ALU.mult, op1=ALU.add,
+                )
+            else:
+                nc.vector.tensor_scalar(
+                    out=bias_t[:], in0=dist_t[:], scalar1=-sigma, scalar2=None, op0=ALU.mult
+                )
+            st["bias", h] = bias_t
+
+        def g_qk_transpose(g):
+            h, half = divmod(g, 2)
+            x = st["x", h // GH]
+            cols = slice((h % GH) * E, (h % GH + 1) * E)
+            qk_ps = ps_a.tile([P, 2 * GT, P], BF16, tag="a", name="qk_ps")
+            for j in range(GT):
+                nc.tensor.transpose(qk_ps[:, j, :], x[:, 4 * half + j, 0, cols], ident_bf[:])
+            for j in range(GT):
+                nc.tensor.transpose(qk_ps[:, GT + j, :], x[:, 4 * half + j, 1, cols], perm_bf[:])
+            st["qk_ps", g] = qk_ps
+
+        def g_qk_copy(g):
+            h, half = divmod(g, 2)
+            qk_ps = st["qk_ps", g]
+            q_t = qpool.tile([P, GT, P], BF16, tag="q_t", name="q_t")
+            nc.scalar.copy(out=q_t[:].bitcast(F32), in_=qk_ps[:, 0:GT, :].bitcast(F32))
+            if half == 0:
+                st["k_t", h] = kpool.tile([P, NQB, P], BF16, tag="k_t", name="k_t")
+            nc.scalar.copy(
+                out=st["k_t", h][:, 4 * half : 4 * half + 4, :].bitcast(F32),
+                in_=qk_ps[:, GT : 2 * GT, :].bitcast(F32),
+            )
+            st["q_t", g] = q_t
 
         def g_window_scores(g):
-            qb, hg = g // 4, g % 4
-            wb = ps_a.tile([P, GH, P], F32, tag="a", name="wb")
-            q_t = st["q_t", g]
-            for j in range(GH):
-                h = GH * hg + j
+            h = g // 2
+            wb = ps_a.tile([P, GT, P], F32, tag="a", name="wb")
+            for j in range(GT):
                 nc.tensor.matmul(
-                    wb[:, j, :], lhsT=bias_t[:, h, 4, :], rhs=perm_f[:],
+                    wb[:, j, :], lhsT=st["bias", h][:, 4, :], rhs=perm_f[:],
                     is_transpose=True, start=True, stop=False,
                 )
                 nc.tensor.matmul(
-                    wb[:, j, :], lhsT=q_t[:, j, :], rhs=k_t[:, h, (qb - 4) * P : (qb - 3) * P],
+                    wb[:, j, :], lhsT=st["q_t", g][:, j, :], rhs=st["k_t", h][:, j, :],
                     start=False, stop=True,
                 )
             st["wb", g] = wb
 
         def g_window_pass(g):
-            mw = gsmall.tile([P, GH], F32, tag="mw", name="mw")
-            for j in range(GH):
+            mw = gsmall.tile([P, GT], F32, tag="mw", name="mw")
+            for j in range(GT):
                 z = zpool.tile([P, 5 * P], F32, tag="z", name="z")
                 nc.vector.tensor_scalar(
                     out=z[:, 0:P], in0=st["wb", g][:, j, :], scalar1=-SCALE, scalar2=None,
                     op0=ALU.mult, op1=ALU.min, accum_out=mw[:, j : j + 1],
                 )
-                st["z", GH * g + j] = z
+                st["z", GT * g + j] = z
             st["mw", g] = mw
 
         def g_mx(g):
-            qb, hg = g // 4, g % 4
-            ob = ps_a.tile([P, GH, P], F32, tag="a", name="ob")
-            for j in range(GH):
-                h = GH * hg + j
-                fcols = slice(h * E, (h + 1) * E)
-                if qb >= 4:
-                    codes, scl = st["codes", GH * g + j]
-                    passes = [(0, 0), (1, 1)]
-                else:
-                    codes, scl = st["codes", GH * g + (j // 2) * 2 + 1]
-                    passes = [(j % 2, 0)]
-                for i, (half, c) in enumerate(passes):
-                    qcols = slice(half * P, (half + 1) * P)
+            h, half = divmod(g, 2)
+            hg = h // GH
+            fcols = slice((h % GH) * E, (h % GH + 1) * E)
+            (v0, s0), (v1, s1) = st["v", hg, 0], st["v", hg, 1]
+            var = vvar[hg % 2]
+            if half == 0:
+                passes = [
+                    [(1, var["moved", 0], vmscales[hg % 2])],
+                    [(0, v0, s0)],
+                    [(1, var["first", 2], s0)],
+                    [(2, v0, s0)],
+                ]
+            else:
+                passes = [
+                    [
+                        (3 + j, var["hi", j] if j else v0, s0),
+                        (4 + j, var["lo", j] if j < 3 else v1, s1),
+                    ]
+                    for j in range(GT)
+                ]
+            ob = ps_a.tile([P, GT, P], F32, tag="a", name="ob")
+            for j in range(GT):
+                for i, (s, vc, vs) in enumerate(passes[j]):
+                    codes, scl = st["codes", h, s // 2]
+                    qcols = slice((s % 2) * P, (s % 2 + 1) * P)
                     nc.tensor.matmul_mx(
                         out=ob[:, j, :],
                         lhsT=codes[:, qcols].bitcast(FP8X4),
                         lhsT_scale=scl[:, qcols],
-                        rhs=vcodes[:, c, fcols].bitcast(FP8X4),
-                        rhs_scale=vscales[:, c, fcols],
+                        rhs=vc[:, fcols].bitcast(FP8X4),
+                        rhs_scale=vs[:, fcols],
                         start=(i == 0),
-                        stop=(i == len(passes) - 1),
+                        stop=(i == len(passes[j]) - 1),
                     )
             st["ob", g] = ob
 
         def g_out(g):
-            qb, hg = g // 4, g % 4
-            rinv = gsmall.tile([P, GH], F32, tag="rinv", name="rinv")
+            h, half = divmod(g, 2)
+            rinv = gsmall.tile([P, GT], F32, tag="rinv", name="rinv")
             nc.vector.reciprocal(out=rinv[:], in_=st["rs", g][:])
-            ost = opool.tile([P, GH, P], F32, tag="ost", name="ost")
+            ost = opool.tile([P, GT, P], F32, tag="ost", name="ost")
             nc.vector.tensor_tensor(
-                out=ost[:], in0=st["ob", g][:], in1=rinv[:].unsqueeze(2).to_broadcast([P, GH, P]),
+                out=ost[:], in0=st["ob", g][:], in1=rinv[:].unsqueeze(2).to_broadcast([P, GT, P]),
                 op=ALU.mult,
             )
-            nc.sync.dma_start(out=out[0, qb * P : (qb + 1) * P, GH * hg : GH * hg + GH, :], in_=ost[:])
+            nc.sync.dma_start(
+                out=out[0, 512 * half : 512 * half + 512, h, :].rearrange("(b p) e -> p b e", p=P), in_=ost[:]
+            )
 
         def t_scores(n):
-            qb, hg, j, h = where(n)
-            nb = min(qb + 1, 4)
+            g, h, half, j, nb = where(n)
+            qb = 4 * half + j
             sb = ps_s.tile([P, 4 * P], F32, tag="s", name="sb")
             for b in range(nb):
                 nc.tensor.matmul(
-                    sb[:, b * P : (b + 1) * P], lhsT=bias_t[:, h, nb - 1 - b, :], rhs=perm_f[:],
+                    sb[:, b * P : (b + 1) * P], lhsT=st["bias", h][:, nb - 1 - b, :], rhs=perm_f[:],
                     is_transpose=True, start=(b == 0), stop=False,
                 )
             nc.tensor.matmul(
-                sb[:, 0 : nb * P], lhsT=st["q_t", n // GH][:, j, :],
-                rhs=k_t[:, h, (qb - nb + 1) * P : (qb + 1) * P], start=False, stop=True,
+                sb[:, 0 : nb * P], lhsT=st["q_t", g][:, j, :],
+                rhs=st["k_t", h][:, qb - nb + 1 : qb + 1, :], start=False, stop=True,
             )
             st["sb", n] = sb
 
         def t_pass(n):
-            qb, hg, j, h = where(n)
-            nb = min(qb + 1, 4)
+            g, h, half, j, nb = where(n)
             nbias = small.tile([P, 1], F32, tag="nbias", name="nbias")
-            if qb >= 4:
+            if half:
                 z = st["z", n]
-                first = st["mw", n // GH][:, j : j + 1]
+                first = st["mw", g][:, j : j + 1]
             else:
                 z = zpool.tile([P, 5 * P], F32, tag="z", name="z")
                 st["z", n] = z
@@ -265,62 +312,51 @@ def tile_flexattention_kernel(tc, qkv, out):
             st["nbias", n] = nbias
 
         def t_exp(n):
-            qb, hg, j, h = where(n)
-            nb = min(qb + 1, 4)
-            g = n // GH
+            g, h, half, j, nb = where(n)
             if j == 0:
-                st["rs", g] = gsmall.tile([P, GH], F32, tag="rs", name="rs")
-            if qb >= 4 or j % 2 == 0:
-                e = es[counters["e"] % N_E]
-                counters["e"] += 1
-                if h < (N_E if qb >= 4 else 0):
-                    if qb == 4:
-                        nc.gpsimd.memset(e[:, :, 5:8, :], 0.0)
-                    else:
-                        nc.gpsimd.memset(e[:, :, qb - 5 : qb - 4, :], 0.0)
-                st["e_now"] = e
-            e = st["e_now"]
-            if qb >= 4:
-                lo, k0, k1 = 0, qb - 4, qb + 1
+                st["rs", g] = gsmall.tile([P, GT], F32, tag="rs", name="rs")
+            e = es[half][h % N_E]
+            if half:
+                lo, slot, width = 0, 5 * j, 5
             else:
-                lo, k0, k1 = P, 4 * (j % 2), 4 * (j % 2) + nb
+                lo, slot, width = P, 4 * HALF0_PLACE[j][0] + HALF0_PLACE[j][1], nb
             nc.scalar.activation(
-                out=e[:, :, k0:k1, :],
+                out=e[:, :, slot : slot + width, :],
                 in_=st["z", n][:, lo : P + nb * P].rearrange("p (b u w) -> p u b w", u=2, w=64),
                 func=ACT.Exp, bias=st["nbias", n][:], scale=-1.0, accum_out=st["rs", g][:, j : j + 1],
             )
-            st["e", n] = e
+
+        SETS = ((), (0,), (1,), (2,), (3,), (4,), (5,), (6, 7))
+        BANKS = (None, None, 0, None, 1, None, 2, 3)
 
         def t_transpose(n):
-            qb, hg, j, h = where(n)
-            if qb >= 4 or j % 2 == 0:
-                st["bank_now"] = tps[counters["tp"] % N_TP]
-                counters["tp"] += 1
-            bank = st["bank_now"]
-            words = st["e", n][:].rearrange("p u k w -> p (u k w)").bitcast(F32)
-            for c in range(2) if qb >= 4 else (j % 2,):
+            g, h, half, j, nb = where(n)
+            words = es[half][h % N_E][:].rearrange("p u s w -> p (u s w)").bitcast(F32)
+            u_words = (20 if half else 12) * 32
+            for s in SETS[4 * half + j]:
+                if s % 2 == 0:
+                    st["bank", h, s // 2] = ps_t.tile([P, 2, 2, P], F32, tag="tp", name="tp")
+                bank = st["bank", h, s // 2]
                 for u in range(2):
-                    first = (2 * u + c) * P
-                    nc.tensor.transpose(bank[:, u, c, :], words[:, first : first + P], ident_f[:])
-            st["bank", n] = bank
+                    first = u * u_words + (s - 3 if half else s) * P
+                    nc.tensor.transpose(bank[:, u, s % 2, :], words[:, first : first + P], ident_f[:])
 
         def t_copy(n):
-            qb, hg, j, h = where(n)
-            if qb < 4 and j % 2 == 0:
+            g, h, half, j, nb = where(n)
+            b = BANKS[4 * half + j]
+            if b is None:
                 return
             grp = gpool.tile([P, 2, P, 4], BF16, tag="grp", name="grp", align_bytes=64)
-            dst = grp[:].rearrange("p c q t -> p (c q t)").bitcast(F32).rearrange("p (c q u) -> p c q u", c=2, u=2)
-            src = st["bank", n][:].rearrange("p u c q -> p c q u")
-            units, u = (8, h // 2) if qb < 4 else (16, h)
-            if (u + 1) * VEC_BANKS[qb] // units > u * VEC_BANKS[qb] // units:
-                nc.vector.tensor_copy(out=dst, in_=src)
-            else:
-                nc.scalar.copy(out=dst, in_=src)
+            nc.scalar.copy(
+                out=grp[:].rearrange("p c q t -> p (c q t)").bitcast(F32).rearrange("p (c q u) -> p c q u", c=2, u=2),
+                in_=st["bank", h, b][:].rearrange("p u c q -> p c q u"),
+            )
             st["grp", n] = grp
 
         def t_quantise(n):
-            qb, hg, j, h = where(n)
-            if qb < 4 and j % 2 == 0:
+            g, h, half, j, nb = where(n)
+            b = BANKS[4 * half + j]
+            if b is None:
                 return
             codes = cpool.tile([P, 2 * P], U32, tag="codes", name="codes", align_bytes=64)
             scl = cpool.tile([P, 2 * P], U8, tag="scl", name="scl", align_bytes=64)
@@ -328,16 +364,26 @@ def tile_flexattention_kernel(tc, qkv, out):
                 out=codes[:].bitcast(FP8X4), scales=scl[:],
                 in_=st["grp", n][:].rearrange("p g q t -> p (g q t)"),
             )
-            st["codes", n] = (codes, scl)
+            st["codes", h, b] = (codes, scl)
 
         def tile_at(s, lag):
             return s - lag if 0 <= s - lag < NT else None
 
-        def group_at(s, off, lo=0, hi=NG):
-            g, r = divmod(s - off, GH)
-            return g if r == 0 and lo <= g < hi else None
+        def group_at(s, off):
+            g, r = divmod(s - off, GT)
+            return g if r == 0 and 0 <= g < NG else None
 
-        for s in range(G_QKT, NT + G_OUT):
+        v_plan = {}
+        for hg in range(NHG):
+            for c in range(2):
+                if hg == 0:
+                    base, (sc, sq) = 0, V_STEPS_FIRST[c]
+                else:
+                    base, (sc, sq) = HGT * (hg - 1), V_STEPS[c]
+                v_plan.setdefault(base + sc, []).append((v_copy, hg, c))
+                v_plan.setdefault(base + sq, []).append((v_quantise, hg, c))
+
+        for s in range(-BIAS_AHEAD, NT + G_OUT):
             n = tile_at(s, 0)
             if n is not None:
                 t_scores(n)
@@ -347,20 +393,20 @@ def tile_flexattention_kernel(tc, qkv, out):
             g = group_at(s, G_QKT)
             if g is not None:
                 g_qk_transpose(g)
-            g = group_at(s, G_W, lo=16)
-            if g is not None:
+            g = group_at(s, G_W)
+            if g is not None and g % 2:
                 g_window_scores(g)
             g = group_at(s, G_MX)
             if g is not None:
                 g_mx(g)
-            g = group_at(s, G_BIAS, hi=4)
-            if g is not None:
-                g_bias(g)
+            g = group_at(s, -BIAS_AHEAD)
+            if g is not None and g % 2 == 0:
+                h_bias(g // 2)
             g = group_at(s, G_QKCOPY)
             if g is not None:
                 g_qk_copy(g)
-            g = group_at(s, G_WPASS, lo=16)
-            if g is not None:
+            g = group_at(s, G_WPASS)
+            if g is not None and g % 2:
                 g_window_pass(g)
             n = tile_at(s, LAG_PASS)
             if n is not None:
@@ -374,14 +420,10 @@ def tile_flexattention_kernel(tc, qkv, out):
             n = tile_at(s, LAG_Q)
             if n is not None:
                 t_quantise(n)
-            g = group_at(s, G_V)
-            if g is not None and g % 16 < 4:
-                g_v(g)
-            g = group_at(s, G_VQ)
-            if g is not None and g % 16 < 4:
-                g_v_quantise(g)
+            for stage, hg, c in v_plan.get(s, []):
+                stage(hg, c)
             g = group_at(s, G_OUT)
             if g is not None:
                 g_out(g)
-            if s % H == 6 and N_X <= s // H + N_X < NQB:
-                load_x(s // H + N_X)
+            if s > 0 and s % HGT == 0 and s // HGT + 1 < NHG:
+                load(s // HGT + 1)

@@ -39,6 +39,10 @@ BIAS_AHEAD = 12
 HALF0_PLACE = ((1, 3), (0, 0), (1, 0), (2, 0))
 
 
+def sigma_of(h):
+    return 2.0 ** (-(h + 1) / 2.0) * math.sqrt(E)
+
+
 def tile_flexattention_kernel(tc, qkv, out):
     nc = tc.nc
     with ExitStack() as ctx:
@@ -94,21 +98,30 @@ def tile_flexattention_kernel(tc, qkv, out):
             out=perm_bf[:].rearrange("p (u r w) -> p u r w", u=2, w=2),
             in_=ident_bf[:].rearrange("p (r u w) -> p u r w", u=2, w=2),
         )
-        dist_t = const.tile([P, 5, P], F32, name="dist_t")
+        key_t = const.tile([P, 2, P], F32, name="key_t")
         nc.gpsimd.iota(
-            dist_t[:],
-            pattern=[[P, 5], [1, P]],
-            base=0,
-            channel_multiplier=-1,
+            key_t[:], pattern=[[-512, 2], [0, P]], base=0, channel_multiplier=1,
             allow_small_or_imprecise_dtypes=True,
         )
         nc.gpsimd.affine_select(
-            out=dist_t[:, 0, :], in_=dist_t[:, 0, :], pattern=[[1, P]],
-            compare_op=ALU.is_ge, fill=MASKED, base=0, channel_multiplier=-1,
+            out=key_t[:, 0, :], in_=key_t[:, 0, :], pattern=[[1, P]],
+            compare_op=ALU.is_ge, fill=-MASKED, base=0, channel_multiplier=-1,
         )
         nc.gpsimd.affine_select(
-            out=dist_t[:, 4, :], in_=dist_t[:, 4, :], pattern=[[-1, P]],
-            compare_op=ALU.is_gt, fill=MASKED, base=0, channel_multiplier=1,
+            out=key_t[:, 1, :], in_=key_t[:, 1, :], pattern=[[-1, P]],
+            compare_op=ALU.is_gt, fill=-MASKED, base=0, channel_multiplier=1,
+        )
+        far_t = const.tile([P, 3, P], F32, name="far_t")
+        nc.gpsimd.iota(
+            far_t[:].rearrange("p b (u r w) -> p b u r w", u=2, w=2),
+            pattern=[[P, 3], [2, 2], [4, 32], [1, 2]], base=-3 * P, channel_multiplier=0,
+            allow_small_or_imprecise_dtypes=True,
+        )
+        part_i = const.tile([P, 1], I32, name="part_i")
+        nc.gpsimd.iota(part_i[:], pattern=[[0, 1]], base=0, channel_multiplier=1)
+        heads_t = const.tile([P, H], F32, name="heads_t")
+        nc.gpsimd.iota(
+            heads_t[:], pattern=[[1, H]], base=0, channel_multiplier=0, allow_small_or_imprecise_dtypes=True
         )
         ident_f = const.tile([P, P], F32, name="ident_f")
         make_identity(nc, ident_f[:])
@@ -117,6 +130,32 @@ def tile_flexattention_kernel(tc, qkv, out):
             out=perm_f[:].rearrange("p (u r w) -> p u r w", u=2, w=2),
             in_=ident_f[:].rearrange("p (r u w) -> p u r w", u=2, w=2),
         )
+        nc.vector.tensor_scalar(out=part_i[:], in0=part_i[:], scalar1=31, scalar2=None, op0=ALU.bitwise_and)
+        part_f = const.tile([P, 1], F32, name="part_f")
+        nc.vector.tensor_copy(out=part_f[:], in_=part_i[:])
+        pick = const.tile([P, H], BF16, name="pick")
+        nc.vector.tensor_scalar(out=pick[:], in0=heads_t[:], scalar1=part_f[:], scalar2=None, op0=ALU.is_equal)
+        sigmas = const.tile([P, H], F32, name="sigmas")
+        for h in range(H):
+            nc.vector.tensor_scalar(
+                out=sigmas[:, h : h + 1], in0=part_f[:], scalar1=float(h), scalar2=sigma_of(h),
+                op0=ALU.is_equal, op1=ALU.mult,
+            )
+        sigma = const.tile([P, 1], F32, name="sigma")
+        nc.vector.reduce_sum(out=sigma[:], in_=sigmas[:], axis=mybir.AxisListType.X)
+        rest = const.tile([P, 3 * P], F32, name="rest")
+        alibi = const.tile([P, 3 * P], BF16, name="alibi")
+        mid = const.tile([P, 3 * P], BF16, name="mid")
+        nc.vector.tensor_scalar(
+            out=rest[:], in0=far_t[:].rearrange("p b c -> p (b c)"), scalar1=sigma[:], scalar2=None, op0=ALU.mult
+        )
+        nc.vector.tensor_copy(out=alibi[:], in_=rest[:])
+        nc.vector.tensor_tensor(out=rest[:], in0=rest[:], in1=alibi[:], op=ALU.subtract)
+        nc.vector.tensor_copy(out=mid[:], in_=rest[:])
+        nc.vector.tensor_tensor(out=rest[:], in0=rest[:], in1=mid[:], op=ALU.subtract)
+        nc.vector.tensor_copy(out=alibi[32:64, :], in_=mid[32:64, :])
+        nc.vector.tensor_copy(out=alibi[64:96, :], in_=rest[64:96, :])
+        nc.vector.memset(alibi[96:128, :], 0.0)
         es = (
             [const.tile([P, 2, 12, 64], BF16, name="ea%d" % i) for i in range(N_E)],
             [const.tile([P, 2, 20, 64], BF16, name="eb%d" % i) for i in range(N_E)],
@@ -169,15 +208,14 @@ def tile_flexattention_kernel(tc, qkv, out):
                 nc.sync.dma_start(out=vmscales[hg % 2][96:100, :].bitcast(I32), in_=scl[0:4, :].bitcast(I32))
 
         def h_bias(h):
-            sigma = 2.0 ** (-(h + 1) / 2.0) * math.sqrt(E)
-            bias_t = bpool.tile([P, 5, P], F32, tag="bias", name="bias_t")
+            bias_t = bpool.tile([P, 2, P], F32, tag="bias", name="bias_t")
             if h > 1:
                 nc.gpsimd.tensor_scalar(
-                    out=bias_t[:], in0=dist_t[:], scalar1=-sigma, scalar2=0.0, op0=ALU.mult, op1=ALU.add,
+                    out=bias_t[:], in0=key_t[:], scalar1=sigma_of(h), scalar2=0.0, op0=ALU.mult, op1=ALU.add,
                 )
             else:
                 nc.vector.tensor_scalar(
-                    out=bias_t[:], in0=dist_t[:], scalar1=-sigma, scalar2=None, op0=ALU.mult
+                    out=bias_t[:], in0=key_t[:], scalar1=sigma_of(h), scalar2=None, op0=ALU.mult
                 )
             st["bias", h] = bias_t
 
@@ -210,7 +248,7 @@ def tile_flexattention_kernel(tc, qkv, out):
             wb = ps_a.tile([P, GT, P], F32, tag="a", name="wb")
             for j in range(GT):
                 nc.tensor.matmul(
-                    wb[:, j, :], lhsT=st["bias", h][:, 4, :], rhs=perm_f[:],
+                    wb[:, j, :], lhsT=st["bias", h][:, 1, :], rhs=perm_f[:],
                     is_transpose=True, start=True, stop=False,
                 )
                 nc.tensor.matmul(
@@ -284,10 +322,15 @@ def tile_flexattention_kernel(tc, qkv, out):
             g, h, half, j, nb = where(n)
             qb = 4 * half + j
             sb = ps_s.tile([P, 4 * P], F32, tag="s", name="sb")
-            for b in range(nb):
+            far = (nb - 1) * P
+            nc.tensor.matmul(
+                sb[:, far : far + P], lhsT=st["bias", h][:, 0, :], rhs=perm_f[:],
+                is_transpose=True, start=True, stop=False,
+            )
+            if far:
                 nc.tensor.matmul(
-                    sb[:, b * P : (b + 1) * P], lhsT=st["bias", h][:, nb - 1 - b, :], rhs=perm_f[:],
-                    is_transpose=True, start=(b == 0), stop=False,
+                    sb[:, 0:far], lhsT=pick[:, h : h + 1].to_broadcast([P, P]), rhs=alibi[:, 3 * P - far : 3 * P],
+                    start=False, stop=False,
                 )
             nc.tensor.matmul(
                 sb[:, 0 : nb * P], lhsT=st["q_t", g][:, j, :],

@@ -21,22 +21,28 @@ NQB = L // P
 GH = 4
 NHG = H // GH
 GT = 4
-NG = 2 * H
-NT = GT * NG
-HGT = NT // NHG
 SCALE = 1.0 / math.sqrt(E)
 MASKED = 1.0e30
 FLOPS = 4 * E * H * (512 * 512 + 512 * 1024)
 
-N_TP = 3
+SCORE_BANKS = (
+    (("m0", 0), ("m1", 0)),
+    (("q3", 0), ("q1", 0)),
+    (("m2", 0), ("m3", 0)),
+    (("q2q0", 0), ("window", 1)),
+)
+EXPS = (("m0", "m1"), ("q3", "q1"), ("m2", "m3"), ("q2", "q0"))
+SLOTS = {"q1": 0, "q2": 4, "q0": 7, "q3": 8, "m0": 0, "m1": 5, "m2": 10, "m3": 15}
+SET_BANKS = (((1, 0), (1, 1)), ((0, 2), (0, 0)), ((1, 2), (1, 3)), ((1, 4), (0, 1)))
+AT_QKT = (-5, -3)
+AT_BIAS = -6
+LAG_PASS, LAG_EXP = 1, 2
+AT_TR = 3
+LAG_Q = 1
+AT_MX = (10, 8)
+V_FIRST = ((0, 1), (2, 3))
+V_NEXT = ((10, 14), (14, 18))
 N_E = 3
-LAG_PASS, LAG_EXP, LAG_TR, LAG_COPY, LAG_Q = 1, 3, 5, 6, 8
-G_QKT, G_QKCOPY, G_W, G_WPASS, G_MX, G_OUT = -8, -6, -1, 0, 17, 18
-V_STEPS = ((15, 17), (19, 21))
-V_STEPS_FIRST = ((2, 3), (5, 6))
-BIAS_AHEAD = 12
-
-HALF0_PLACE = ((1, 3), (0, 0), (1, 0), (2, 0))
 
 
 def sigma_of(h):
@@ -51,30 +57,30 @@ def tile_flexattention_kernel(tc, qkv, out):
         ld = ctx.enter_context(tc.tile_pool(name="ld", bufs=2))
         bpool = ctx.enter_context(tc.tile_pool(name="bpool", bufs=4))
         kpool = ctx.enter_context(tc.tile_pool(name="kpool", bufs=4))
-        qpool = ctx.enter_context(tc.tile_pool(name="qpool", bufs=4))
+        qpool = ctx.enter_context(tc.tile_pool(name="qpool", bufs=8))
         vpool = ctx.enter_context(tc.tile_pool(name="vpool", bufs=2))
-        small = ctx.enter_context(tc.tile_pool(name="small", bufs=8))
+        small = ctx.enter_context(tc.tile_pool(name="small", bufs=16))
         gsmall = ctx.enter_context(tc.tile_pool(name="gsmall", bufs=8))
         zpool = ctx.enter_context(tc.tile_pool(name="zpool", bufs=8))
         gpool = ctx.enter_context(tc.tile_pool(name="gpool", bufs=4))
-        cpool = ctx.enter_context(tc.tile_pool(name="cpool", bufs=12))
-        opool = ctx.enter_context(tc.tile_pool(name="opool", bufs=3))
-        ps_s = ctx.enter_context(tc.psum_pool(name="ps_s", bufs=3))
-        ps_t = ctx.enter_context(tc.psum_pool(name="ps_t", bufs=N_TP))
+        cpool = ctx.enter_context(tc.tile_pool(name="cpool", bufs=14))
+        opool = ctx.enter_context(tc.tile_pool(name="opool", bufs=4))
+        ps_s = ctx.enter_context(tc.psum_pool(name="ps_s", bufs=4))
+        ps_t = ctx.enter_context(tc.psum_pool(name="ps_t", bufs=2))
         ps_a = ctx.enter_context(tc.psum_pool(name="ps_a", bufs=2))
 
         st = {}
 
-        qksrc = qkv[0].rearrange("(b p) w h e -> p b w (h e)", p=P)
+        qksrc = qkv[0].rearrange("(b p) w h e -> p w b (h e)", p=P)
         vsrc = qkv[0, :, 2].rearrange("(c p t) h e -> p c t (h e)", p=P, t=4)
 
-        def load_qk(hg, half):
-            if half == 0:
-                st["x", hg] = ld.tile([P, NQB, 2, GH * E], BF16, tag="x", name="x")
-            for b in range(4 * half, 4 * half + 4):
-                nc.sync.dma_start(
-                    out=st["x", hg][:, b], in_=qksrc[:, b, 0:2, hg * GH * E : (hg + 1) * GH * E]
-                )
+        def load_qk(hg, w, h0=0, h1=GH):
+            if w == 0 and h0 == 0:
+                st["x", hg] = ld.tile([P, 2, NQB, GH * E], BF16, tag="x", name="x")
+            nc.sync.dma_start(
+                out=st["x", hg][:, w, :, h0 * E : h1 * E],
+                in_=qksrc[:, w, :, (hg * GH + h0) * E : (hg * GH + h1) * E],
+            )
 
         def load_v(hg, c):
             if c == 0:
@@ -83,13 +89,12 @@ def tile_flexattention_kernel(tc, qkv, out):
                 out=st["vraw", hg][:, c], in_=vsrc[:, c, :, hg * GH * E : (hg + 1) * GH * E]
             )
 
-        def load(hg):
-            for half in range(2):
-                load_qk(hg, half)
-                load_v(hg, half)
-
-        load(0)
-        load(1)
+        load_qk(0, 0, 0, 1)
+        load_qk(0, 1, 0, 1)
+        load_v(0, 0)
+        load_qk(0, 0, 1, GH)
+        load_qk(0, 1, 1, GH)
+        load_v(0, 1)
 
         ident_bf = const.tile([P, P], BF16, name="ident_bf")
         make_identity(nc, ident_bf[:])
@@ -97,6 +102,13 @@ def tile_flexattention_kernel(tc, qkv, out):
         nc.vector.tensor_copy(
             out=perm_bf[:].rearrange("p (u r w) -> p u r w", u=2, w=2),
             in_=ident_bf[:].rearrange("p (r u w) -> p u r w", u=2, w=2),
+        )
+        ident_f = const.tile([P, P], F32, name="ident_f")
+        make_identity(nc, ident_f[:])
+        perm_f = const.tile([P, P], F32, name="perm_f")
+        nc.vector.tensor_copy(
+            out=perm_f[:].rearrange("p (u r w) -> p u r w", u=2, w=2),
+            in_=ident_f[:].rearrange("p (r u w) -> p u r w", u=2, w=2),
         )
         key_t = const.tile([P, 2, P], F32, name="key_t")
         nc.gpsimd.iota(
@@ -111,25 +123,32 @@ def tile_flexattention_kernel(tc, qkv, out):
             out=key_t[:, 1, :], in_=key_t[:, 1, :], pattern=[[-1, P]],
             compare_op=ALU.is_gt, fill=-MASKED, base=0, channel_multiplier=1,
         )
-        far_t = const.tile([P, 3, P], F32, name="far_t")
-        nc.gpsimd.iota(
-            far_t[:].rearrange("p b (u r w) -> p b u r w", u=2, w=2),
-            pattern=[[P, 3], [2, 2], [4, 32], [1, 2]], base=-3 * P, channel_multiplier=0,
-            allow_small_or_imprecise_dtypes=True,
-        )
         part_i = const.tile([P, 1], I32, name="part_i")
         nc.gpsimd.iota(part_i[:], pattern=[[0, 1]], base=0, channel_multiplier=1)
         heads_t = const.tile([P, H], F32, name="heads_t")
         nc.gpsimd.iota(
             heads_t[:], pattern=[[1, H]], base=0, channel_multiplier=0, allow_small_or_imprecise_dtypes=True
         )
-        ident_f = const.tile([P, P], F32, name="ident_f")
-        make_identity(nc, ident_f[:])
-        perm_f = const.tile([P, P], F32, name="perm_f")
-        nc.vector.tensor_copy(
-            out=perm_f[:].rearrange("p (u r w) -> p u r w", u=2, w=2),
-            in_=ident_f[:].rearrange("p (r u w) -> p u r w", u=2, w=2),
+        far_t = const.tile([P, 3, P], F32, name="far_t")
+        nc.gpsimd.iota(
+            far_t[:].rearrange("p b (u r w) -> p b u r w", u=2, w=2),
+            pattern=[[P, 3], [2, 2], [4, 32], [1, 2]], base=-3 * P, channel_multiplier=0,
+            allow_small_or_imprecise_dtypes=True,
         )
+
+        def h_bias(h):
+            bias_t = bpool.tile([P, 2, P], F32, tag="bias", name="bias_t")
+            if h:
+                nc.gpsimd.tensor_scalar(
+                    out=bias_t[:], in0=key_t[:], scalar1=sigma_of(h), scalar2=0.0, op0=ALU.mult, op1=ALU.add,
+                )
+            else:
+                nc.vector.tensor_scalar(
+                    out=bias_t[:], in0=key_t[:], scalar1=sigma_of(h), scalar2=None, op0=ALU.mult
+                )
+            st["bias", h] = bias_t
+
+        h_bias(0)
         nc.vector.tensor_scalar(out=part_i[:], in0=part_i[:], scalar1=31, scalar2=None, op0=ALU.bitwise_and)
         part_f = const.tile([P, 1], F32, name="part_f")
         nc.vector.tensor_copy(out=part_f[:], in_=part_i[:])
@@ -172,15 +191,11 @@ def tile_flexattention_kernel(tc, qkv, out):
             for i in range(2)
         ]
         vmscales = [const.tile([P, GH * E], U8, name="vms%d" % i, align_bytes=64) for i in range(2)]
-        for i in range(2):
-            for key in VARIANTS:
-                nc.gpsimd.memset(vvar[i][key][:], 0)
-            nc.gpsimd.memset(vmscales[i][:].bitcast(U32), 0)
 
-        def where(n):
-            g, j = divmod(n, GT)
-            h, half = divmod(g, 2)
-            return g, h, half, j, (4 if half else j + 1)
+        def zero_variants(i, engine):
+            for key in VARIANTS:
+                engine.memset(vvar[i][key][:], 0)
+            engine.memset(vmscales[i][:].bitcast(U32), 0)
 
         def v_copy(hg, c):
             gv = vpool.tile([P, GH * E, 4], BF16, tag="gv", name="gv", align_bytes=64)
@@ -207,69 +222,70 @@ def tile_flexattention_kernel(tc, qkv, out):
             if c == 0:
                 nc.sync.dma_start(out=vmscales[hg % 2][96:100, :].bitcast(I32), in_=scl[0:4, :].bitcast(I32))
 
-        def h_bias(h):
-            bias_t = bpool.tile([P, 2, P], F32, tag="bias", name="bias_t")
-            if h > 1:
-                nc.gpsimd.tensor_scalar(
-                    out=bias_t[:], in0=key_t[:], scalar1=sigma_of(h), scalar2=0.0, op0=ALU.mult, op1=ALU.add,
-                )
-            else:
-                nc.vector.tensor_scalar(
-                    out=bias_t[:], in0=key_t[:], scalar1=sigma_of(h), scalar2=None, op0=ALU.mult
-                )
-            st["bias", h] = bias_t
-
-        def g_qk_transpose(g):
-            h, half = divmod(g, 2)
+        def qk_transpose(h, half):
             x = st["x", h // GH]
             cols = slice((h % GH) * E, (h % GH + 1) * E)
             qk_ps = ps_a.tile([P, 2 * GT, P], BF16, tag="a", name="qk_ps")
             for j in range(GT):
-                nc.tensor.transpose(qk_ps[:, j, :], x[:, 4 * half + j, 0, cols], ident_bf[:])
+                nc.tensor.transpose(qk_ps[:, j, :], x[:, 0, GT * half + j, cols], ident_bf[:])
             for j in range(GT):
-                nc.tensor.transpose(qk_ps[:, GT + j, :], x[:, 4 * half + j, 1, cols], perm_bf[:])
-            st["qk_ps", g] = qk_ps
+                nc.tensor.transpose(qk_ps[:, GT + j, :], x[:, 1, GT * half + j, cols], perm_bf[:])
+            st["qk_ps", h, half] = qk_ps
 
-        def g_qk_copy(g):
-            h, half = divmod(g, 2)
-            qk_ps = st["qk_ps", g]
-            q_t = qpool.tile([P, GT, P], BF16, tag="q_t", name="q_t")
-            nc.scalar.copy(out=q_t[:].bitcast(F32), in_=qk_ps[:, 0:GT, :].bitcast(F32))
-            if half == 0:
-                st["k_t", h] = kpool.tile([P, NQB, P], BF16, tag="k_t", name="k_t")
-            nc.scalar.copy(
-                out=st["k_t", h][:, 4 * half : 4 * half + 4, :].bitcast(F32),
-                in_=qk_ps[:, GT : 2 * GT, :].bitcast(F32),
-            )
-            st["q_t", g] = q_t
+        def e_transpose(h, b):
+            bank = ps_t.tile([P, 2, 2, P], F32, tag="tp", name="tp")
+            for i, (half, s) in enumerate(SET_BANKS[b]):
+                words = es[half][h % N_E][:].rearrange("p u s w -> p (u s w)").bitcast(F32)
+                u_words = (20 if half else 12) * 32
+                for u in range(2):
+                    first = u * u_words + s * P
+                    nc.tensor.transpose(bank[:, u, i, :], words[:, first : first + P], ident_f[:])
+            st["bank", h, b] = bank
 
-        def g_window_scores(g):
-            h = g // 2
-            wb = ps_a.tile([P, GT, P], F32, tag="a", name="wb")
-            for j in range(GT):
+        def masks(h, bank):
+            sb = ps_s.tile([P, 4 * P], F32, tag="s", name="sb")
+            if bank == "window":
+                blocks = range(4)
+            else:
+                blocks = {"q1": (1,), "q2q0": (2, 3)}.get(bank, (3,))
+            for i, b in enumerate(blocks):
                 nc.tensor.matmul(
-                    wb[:, j, :], lhsT=st["bias", h][:, 1, :], rhs=perm_f[:],
-                    is_transpose=True, start=True, stop=False,
+                    sb[:, b * P : (b + 1) * P], lhsT=st["bias", h][:, int(bank == "window"), :], rhs=perm_f[:],
+                    is_transpose=True, start=(i == 0), stop=False,
                 )
+            st["sb", h, bank] = sb
+
+        def scores(h, bank):
+            sb = st["sb", h, bank]
+            k_t = st["k_t", h]
+
+            def product(col, qb, k0, k1, stop):
                 nc.tensor.matmul(
-                    wb[:, j, :], lhsT=st["q_t", g][:, j, :], rhs=st["k_t", h][:, j, :],
-                    start=False, stop=True,
+                    sb[:, col * P : (col + k1 - k0) * P], lhsT=st["q_t", h, qb // GT][:, qb % GT, :],
+                    rhs=k_t[:, k0:k1, :], start=False, stop=stop,
                 )
-            st["wb", g] = wb
 
-        def g_window_pass(g):
-            mw = gsmall.tile([P, GT], F32, tag="mw", name="mw")
-            for j in range(GT):
-                z = zpool.tile([P, 5 * P], F32, tag="z", name="z")
-                nc.vector.tensor_scalar(
-                    out=z[:, 0:P], in0=st["wb", g][:, j, :], scalar1=-SCALE, scalar2=None,
-                    op0=ALU.mult, op1=ALU.min, accum_out=mw[:, j : j + 1],
+            def far(n):
+                nc.tensor.matmul(
+                    sb[:, 0 : n * P], lhsT=pick[:, h : h + 1].to_broadcast([P, P]),
+                    rhs=alibi[:, (3 - n) * P : 3 * P], start=False, stop=False,
                 )
-                st["z", GT * g + j] = z
-            st["mw", g] = mw
 
-        def g_mx(g):
-            h, half = divmod(g, 2)
+            if bank == "window":
+                for j in range(GT):
+                    product(j, GT + j, j, j + 1, j == GT - 1)
+            elif bank == "q2q0":
+                far(2)
+                product(3, 0, 0, 1, False)
+                product(0, 2, 0, 3, True)
+            else:
+                j = int(bank[1])
+                qb = j + (GT if bank[0] == "m" else 0)
+                k0 = max(0, qb - 3)
+                far(qb - k0)
+                product(0, qb, k0, qb + 1, True)
+
+        def mx(h, half):
             hg = h // GH
             fcols = slice((h % GH) * E, (h % GH + 1) * E)
             (v0, s0), (v1, s1) = st["v", hg, 0], st["v", hg, 1]
@@ -283,17 +299,13 @@ def tile_flexattention_kernel(tc, qkv, out):
                 ]
             else:
                 passes = [
-                    [
-                        (3 + j, var["hi", j] if j else v0, s0),
-                        (4 + j, var["lo", j] if j < 3 else v1, s1),
-                    ]
+                    [(j, var["hi", j] if j else v0, s0), (j + 1, var["lo", j] if j < 3 else v1, s1)]
                     for j in range(GT)
                 ]
             ob = ps_a.tile([P, GT, P], F32, tag="a", name="ob")
             for j in range(GT):
                 for i, (s, vc, vs) in enumerate(passes[j]):
-                    codes, scl = st["codes", h, s // 2]
-                    qcols = slice((s % 2) * P, (s % 2 + 1) * P)
+                    codes, scl, qcols = st["codes", h, half, s]
                     nc.tensor.matmul_mx(
                         out=ob[:, j, :],
                         lhsT=codes[:, qcols].bitcast(FP8X4),
@@ -303,170 +315,153 @@ def tile_flexattention_kernel(tc, qkv, out):
                         start=(i == 0),
                         stop=(i == len(passes[j]) - 1),
                     )
-            st["ob", g] = ob
+            st["ob", h, half] = ob
 
-        def g_out(g):
-            h, half = divmod(g, 2)
+        def score_pass(h, bank):
+            sb = st["sb", h, bank]
+
+            def one(z_out, col, n, first, least):
+                nc.vector.tensor_scalar(
+                    out=z_out, in0=sb[:, col * P : (col + n) * P], scalar1=-SCALE, scalar2=first,
+                    op0=ALU.mult, op1=ALU.min, accum_out=least,
+                )
+
+            if bank == "window":
+                mw = gsmall.tile([P, GT], F32, tag="mw", name="mw")
+                for j in range(GT):
+                    z = zpool.tile([P, 5 * P], F32, tag="zm", name="z")
+                    one(z[:, 0:P], j, 1, None, mw[:, j : j + 1])
+                    st["z", h, "m%d" % j] = z
+                    st["first", h, "m%d" % j] = mw[:, j : j + 1]
+                return
+            parts = {"q1": (("q1", 0, 2),), "q2q0": (("q2", 0, 3), ("q0", 3, 1))}.get(bank, ((bank, 0, 4),))
+            for tile, col, n in parts:
+                nbias = small.tile([P, 1], F32, tag="nbias", name="nbias")
+                if tile[0] == "m":
+                    one(st["z", h, tile][:, P : 5 * P], col, n, st["first", h, tile], nbias[:])
+                else:
+                    z = zpool.tile([P, 4 * P], F32, tag="zq", name="z")
+                    one(z[:, 0 : n * P], col, n, None, nbias[:])
+                    st["z", h, tile] = z
+                st["nbias", h, tile] = nbias
+
+        def quantise(h, b):
+            codes = cpool.tile([P, 2 * P], U32, tag="codes", name="codes", align_bytes=64)
+            scl = cpool.tile([P, 2 * P], U8, tag="scl", name="scl", align_bytes=64)
+            nc.vector.quantize_mx(
+                out=codes[:].bitcast(FP8X4), scales=scl[:],
+                in_=st["grp", h, b][:].rearrange("p g q t -> p (g q t)"),
+            )
+            for i, (half, s) in enumerate(SET_BANKS[b]):
+                st["codes", h, half, s] = (codes, scl, slice(i * P, (i + 1) * P))
+
+        def store(h, half):
             rinv = gsmall.tile([P, GT], F32, tag="rinv", name="rinv")
-            nc.vector.reciprocal(out=rinv[:], in_=st["rs", g][:])
+            nc.vector.reciprocal(out=rinv[:], in_=st["rs", h, half][:])
             ost = opool.tile([P, GT, P], F32, tag="ost", name="ost")
             nc.vector.tensor_tensor(
-                out=ost[:], in0=st["ob", g][:], in1=rinv[:].unsqueeze(2).to_broadcast([P, GT, P]),
+                out=ost[:], in0=st["ob", h, half][:], in1=rinv[:].unsqueeze(2).to_broadcast([P, GT, P]),
                 op=ALU.mult,
             )
             nc.sync.dma_start(
                 out=out[0, 512 * half : 512 * half + 512, h, :].rearrange("(b p) e -> p b e", p=P), in_=ost[:]
             )
 
-        def t_scores(n):
-            g, h, half, j, nb = where(n)
-            qb = 4 * half + j
-            sb = ps_s.tile([P, 4 * P], F32, tag="s", name="sb")
-            far = (nb - 1) * P
-            nc.tensor.matmul(
-                sb[:, far : far + P], lhsT=st["bias", h][:, 0, :], rhs=perm_f[:],
-                is_transpose=True, start=True, stop=False,
-            )
-            if far:
-                nc.tensor.matmul(
-                    sb[:, 0:far], lhsT=pick[:, h : h + 1].to_broadcast([P, P]), rhs=alibi[:, 3 * P - far : 3 * P],
-                    start=False, stop=False,
-                )
-            nc.tensor.matmul(
-                sb[:, 0 : nb * P], lhsT=st["q_t", g][:, j, :],
-                rhs=st["k_t", h][:, qb - nb + 1 : qb + 1, :], start=False, stop=True,
-            )
-            st["sb", n] = sb
-
-        def t_pass(n):
-            g, h, half, j, nb = where(n)
-            nbias = small.tile([P, 1], F32, tag="nbias", name="nbias")
-            if half:
-                z = st["z", n]
-                first = st["mw", g][:, j : j + 1]
-            else:
-                z = zpool.tile([P, 5 * P], F32, tag="z", name="z")
-                st["z", n] = z
-                first = None
-            nc.vector.tensor_scalar(
-                out=z[:, P : P + nb * P], in0=st["sb", n][:, 0 : nb * P], scalar1=-SCALE, scalar2=first,
-                op0=ALU.mult, op1=ALU.min, accum_out=nbias[:],
-            )
-            st["nbias", n] = nbias
-
-        def t_exp(n):
-            g, h, half, j, nb = where(n)
-            if j == 0:
-                st["rs", g] = gsmall.tile([P, GT], F32, tag="rs", name="rs")
-            e = es[half][h % N_E]
-            if half:
-                lo, slot, width = 0, 5 * j, 5
-            else:
-                lo, slot, width = P, 4 * HALF0_PLACE[j][0] + HALF0_PLACE[j][1], nb
+        def exp(h, tile):
+            half, j = int(tile[0] == "m"), int(tile[1])
+            if ("rs", h, half) not in st:
+                st["rs", h, half] = gsmall.tile([P, GT], F32, tag="rs%d" % half, name="rs")
+            n = 5 if half else j + 1
             nc.scalar.activation(
-                out=e[:, :, slot : slot + width, :],
-                in_=st["z", n][:, lo : P + nb * P].rearrange("p (b u w) -> p u b w", u=2, w=64),
-                func=ACT.Exp, bias=st["nbias", n][:], scale=-1.0, accum_out=st["rs", g][:, j : j + 1],
+                out=es[half][h % N_E][:, :, SLOTS[tile] : SLOTS[tile] + n, :],
+                in_=st["z", h, tile][:, 0 : n * P].rearrange("p (b u w) -> p u b w", u=2, w=64),
+                func=ACT.Exp, bias=st["nbias", h, tile][:], scale=-1.0,
+                accum_out=st["rs", h, half][:, j : j + 1],
             )
 
-        SETS = ((), (0,), (1,), (2,), (3,), (4,), (5,), (6, 7))
-        BANKS = (None, None, 0, None, 1, None, 2, 3)
-
-        def t_transpose(n):
-            g, h, half, j, nb = where(n)
-            words = es[half][h % N_E][:].rearrange("p u s w -> p (u s w)").bitcast(F32)
-            u_words = (20 if half else 12) * 32
-            for s in SETS[4 * half + j]:
-                if s % 2 == 0:
-                    st["bank", h, s // 2] = ps_t.tile([P, 2, 2, P], F32, tag="tp", name="tp")
-                bank = st["bank", h, s // 2]
-                for u in range(2):
-                    first = u * u_words + (s - 3 if half else s) * P
-                    nc.tensor.transpose(bank[:, u, s % 2, :], words[:, first : first + P], ident_f[:])
-
-        def t_copy(n):
-            g, h, half, j, nb = where(n)
-            b = BANKS[4 * half + j]
-            if b is None:
-                return
+        def e_copy(h, b):
             grp = gpool.tile([P, 2, P, 4], BF16, tag="grp", name="grp", align_bytes=64)
             nc.scalar.copy(
                 out=grp[:].rearrange("p c q t -> p (c q t)").bitcast(F32).rearrange("p (c q u) -> p c q u", c=2, u=2),
                 in_=st["bank", h, b][:].rearrange("p u c q -> p c q u"),
             )
-            st["grp", n] = grp
+            st["grp", h, b] = grp
 
-        def t_quantise(n):
-            g, h, half, j, nb = where(n)
-            b = BANKS[4 * half + j]
-            if b is None:
-                return
-            codes = cpool.tile([P, 2 * P], U32, tag="codes", name="codes", align_bytes=64)
-            scl = cpool.tile([P, 2 * P], U8, tag="scl", name="scl", align_bytes=64)
-            nc.vector.quantize_mx(
-                out=codes[:].bitcast(FP8X4), scales=scl[:],
-                in_=st["grp", n][:].rearrange("p g q t -> p (g q t)"),
+        def qk_copy(h, half):
+            qk_ps = st["qk_ps", h, half]
+            q_t = qpool.tile([P, GT, P], BF16, tag="q_t", name="q_t")
+            nc.scalar.copy(out=q_t[:].bitcast(F32), in_=qk_ps[:, 0:GT, :].bitcast(F32))
+            if half == 0:
+                st["k_t", h] = kpool.tile([P, NQB, P], BF16, tag="k_t", name="k_t")
+            nc.scalar.copy(
+                out=st["k_t", h][:, GT * half : GT * half + GT, :].bitcast(F32),
+                in_=qk_ps[:, GT : 2 * GT, :].bitcast(F32),
             )
-            st["codes", h, b] = (codes, scl)
+            st["q_t", h, half] = q_t
 
-        def tile_at(s, lag):
-            return s - lag if 0 <= s - lag < NT else None
+        def score_banks(k):
+            h, p = divmod(k, 4)
+            return [(h + dh, bank) for bank, dh in SCORE_BANKS[p] if 0 <= h + dh < H and 0 <= h + 1]
 
-        def group_at(s, off):
-            g, r = divmod(s - off, GT)
-            return g if r == 0 and 0 <= g < NG else None
+        def head_at(k, at):
+            h, r = divmod(k - at, 4)
+            return h if r == 0 and 0 <= h < H else None
+
+        def set_bank_at(k):
+            h, b = divmod(k - AT_TR, 4)
+            return (h, b) if 0 <= h < H else None
 
         v_plan = {}
         for hg in range(NHG):
             for c in range(2):
-                if hg == 0:
-                    base, (sc, sq) = 0, V_STEPS_FIRST[c]
-                else:
-                    base, (sc, sq) = HGT * (hg - 1), V_STEPS[c]
-                v_plan.setdefault(base + sc, []).append((v_copy, hg, c))
-                v_plan.setdefault(base + sq, []).append((v_quantise, hg, c))
+                base, (at_copy, at_q) = (0, V_FIRST[c]) if hg == 0 else (16 * (hg - 1), V_NEXT[c])
+                v_plan.setdefault(base + at_copy, []).append((v_copy, hg, c))
+                v_plan.setdefault(base + at_q, []).append((v_quantise, hg, c))
 
-        for s in range(-BIAS_AHEAD, NT + G_OUT):
-            n = tile_at(s, 0)
-            if n is not None:
-                t_scores(n)
-            n = tile_at(s, LAG_TR)
-            if n is not None:
-                t_transpose(n)
-            g = group_at(s, G_QKT)
-            if g is not None:
-                g_qk_transpose(g)
-            g = group_at(s, G_W)
-            if g is not None and g % 2:
-                g_window_scores(g)
-            g = group_at(s, G_MX)
-            if g is not None:
-                g_mx(g)
-            g = group_at(s, -BIAS_AHEAD)
-            if g is not None and g % 2 == 0:
-                h_bias(g // 2)
-            g = group_at(s, G_QKCOPY)
-            if g is not None:
-                g_qk_copy(g)
-            g = group_at(s, G_WPASS)
-            if g is not None and g % 2:
-                g_window_pass(g)
-            n = tile_at(s, LAG_PASS)
-            if n is not None:
-                t_pass(n)
-            n = tile_at(s, LAG_EXP)
-            if n is not None:
-                t_exp(n)
-            n = tile_at(s, LAG_COPY)
-            if n is not None:
-                t_copy(n)
-            n = tile_at(s, LAG_Q)
-            if n is not None:
-                t_quantise(n)
-            for stage, hg, c in v_plan.get(s, []):
+        for k in range(AT_BIAS, 4 * H + AT_MX[0] + 2):
+            if set_bank_at(k):
+                e_transpose(*set_bank_at(k))
+            for half in range(2):
+                h = head_at(k, AT_QKT[half])
+                if h is not None:
+                    qk_transpose(h, half)
+            for h, bank in score_banks(k):
+                masks(h, bank)
+            for h, bank in score_banks(k):
+                scores(h, bank)
+            for half in (1, 0):
+                h = head_at(k, AT_MX[half])
+                if h is not None:
+                    mx(h, half)
+            h = head_at(k, AT_BIAS)
+            if h:
+                h_bias(h)
+            if k == 1:
+                zero_variants(1, nc.gpsimd)
+            if k == AT_QKT[1]:
+                zero_variants(0, nc.vector)
+            for h, bank in score_banks(k - LAG_PASS):
+                score_pass(h, bank)
+            if set_bank_at(k - LAG_Q):
+                quantise(*set_bank_at(k - LAG_Q))
+            for half in (1, 0):
+                h = head_at(k, AT_MX[half] + 1)
+                if h is not None:
+                    store(h, half)
+            for stage, hg, c in v_plan.get(k, []):
                 stage(hg, c)
-            g = group_at(s, G_OUT)
-            if g is not None:
-                g_out(g)
-            if s > 0 and s % HGT == 0 and s // HGT + 1 < NHG:
-                load(s // HGT + 1)
+            if 0 <= k - LAG_EXP < 4 * H:
+                for tile in EXPS[(k - LAG_EXP) % 4]:
+                    exp((k - LAG_EXP) // 4, tile)
+            if set_bank_at(k):
+                e_copy(*set_bank_at(k))
+            for half in range(2):
+                h = head_at(k, AT_QKT[half])
+                if h is not None:
+                    qk_copy(h, half)
+            hg, r = divmod(k + 12, 16)
+            if 1 <= hg < NHG and r < 4:
+                if r < 2:
+                    load_qk(hg, r)
+                else:
+                    load_v(hg, r - 2)

@@ -57,13 +57,12 @@ def tile_flexattention_kernel(tc, qkv, out):
         ld = ctx.enter_context(tc.tile_pool(name="ld", bufs=2))
         bpool = ctx.enter_context(tc.tile_pool(name="bpool", bufs=4))
         kpool = ctx.enter_context(tc.tile_pool(name="kpool", bufs=4))
-        qpool = ctx.enter_context(tc.tile_pool(name="qpool", bufs=8))
         vpool = ctx.enter_context(tc.tile_pool(name="vpool", bufs=2))
         small = ctx.enter_context(tc.tile_pool(name="small", bufs=16))
         gsmall = ctx.enter_context(tc.tile_pool(name="gsmall", bufs=8))
         zpool = ctx.enter_context(tc.tile_pool(name="zpool", bufs=8))
         gpool = ctx.enter_context(tc.tile_pool(name="gpool", bufs=4))
-        cpool = ctx.enter_context(tc.tile_pool(name="cpool", bufs=14))
+        cpool = ctx.enter_context(tc.tile_pool(name="cpool", bufs=8))
         opool = ctx.enter_context(tc.tile_pool(name="opool", bufs=4))
         ps_s = ctx.enter_context(tc.psum_pool(name="ps_s", bufs=4))
         ps_t = ctx.enter_context(tc.psum_pool(name="ps_t", bufs=2))
@@ -91,9 +90,9 @@ def tile_flexattention_kernel(tc, qkv, out):
 
         load_qk(0, 0, 0, 1)
         load_qk(0, 1, 0, 1)
-        load_v(0, 0)
         load_qk(0, 0, 1, GH)
         load_qk(0, 1, 1, GH)
+        load_v(0, 0)
         load_v(0, 1)
 
         ident_bf = const.tile([P, P], BF16, name="ident_bf")
@@ -180,7 +179,7 @@ def tile_flexattention_kernel(tc, qkv, out):
             [const.tile([P, 2, 20, 64], BF16, name="eb%d" % i) for i in range(N_E)],
         )
         for e in es[0]:
-            nc.vector.memset(e[:, :, 2:4, :], 0.0)
+            nc.gpsimd.memset(e[:, :, 2:4, :], 0.0)
         VARIANTS = {
             ("hi", 1): (0, 32, 128), ("hi", 2): (0, 64, 128), ("hi", 3): (0, 96, 128),
             ("lo", 0): (1, 0, 32), ("lo", 1): (1, 0, 64), ("lo", 2): (1, 0, 96),
@@ -192,10 +191,10 @@ def tile_flexattention_kernel(tc, qkv, out):
         ]
         vmscales = [const.tile([P, GH * E], U8, name="vms%d" % i, align_bytes=64) for i in range(2)]
 
-        def zero_variants(i, engine):
+        def zero_variants(i):
             for key in VARIANTS:
-                engine.memset(vvar[i][key][:], 0)
-            engine.memset(vmscales[i][:].bitcast(U32), 0)
+                nc.gpsimd.memset(vvar[i][key][:], 0)
+            nc.gpsimd.memset(vmscales[i][:].bitcast(U32), 0)
 
         def v_copy(hg, c):
             gv = vpool.tile([P, GH * E, 4], BF16, tag="gv", name="gv", align_bytes=64)
@@ -222,14 +221,17 @@ def tile_flexattention_kernel(tc, qkv, out):
             if c == 0:
                 nc.sync.dma_start(out=vmscales[hg % 2][96:100, :].bitcast(I32), in_=scl[0:4, :].bitcast(I32))
 
+        Q_AT, K_AT = (0, 3 * GT), (GT, 2 * GT)
+
         def qk_transpose(h, half):
             x = st["x", h // GH]
             cols = slice((h % GH) * E, (h % GH + 1) * E)
             qk_ps = ps_a.tile([P, 2 * GT, P], BF16, tag="a", name="qk_ps")
-            for j in range(GT):
-                nc.tensor.transpose(qk_ps[:, j, :], x[:, 0, GT * half + j, cols], ident_bf[:])
-            for j in range(GT):
-                nc.tensor.transpose(qk_ps[:, GT + j, :], x[:, 1, GT * half + j, cols], perm_bf[:])
+            for w, at, order in ((0, Q_AT, ident_bf), (1, K_AT, perm_bf)):
+                for j in range(GT):
+                    nc.tensor.transpose(
+                        qk_ps[:, at[half] - 2 * GT * half + j, :], x[:, w, GT * half + j, cols], order[:]
+                    )
             st["qk_ps", h, half] = qk_ps
 
         def e_transpose(h, b):
@@ -257,12 +259,12 @@ def tile_flexattention_kernel(tc, qkv, out):
 
         def scores(h, bank):
             sb = st["sb", h, bank]
-            k_t = st["k_t", h]
+            qk_t = st["qk_t", h]
 
             def product(col, qb, k0, k1, stop):
                 nc.tensor.matmul(
-                    sb[:, col * P : (col + k1 - k0) * P], lhsT=st["q_t", h, qb // GT][:, qb % GT, :],
-                    rhs=k_t[:, k0:k1, :], start=False, stop=stop,
+                    sb[:, col * P : (col + k1 - k0) * P], lhsT=qk_t[:, Q_AT[qb // GT] + qb % GT, :],
+                    rhs=qk_t[:, K_AT[0] + k0 : K_AT[0] + k1, :], start=False, stop=stop,
                 )
 
             def far(n):
@@ -346,21 +348,25 @@ def tile_flexattention_kernel(tc, qkv, out):
                 st["nbias", h, tile] = nbias
 
         def quantise(h, b):
-            codes = cpool.tile([P, 2 * P], U32, tag="codes", name="codes", align_bytes=64)
-            scl = cpool.tile([P, 2 * P], U8, tag="scl", name="scl", align_bytes=64)
+            if b % 2 == 0:
+                return
+            codes = cpool.tile([P, 4 * P], U32, tag="codes", name="codes", align_bytes=64)
+            scl = cpool.tile([P, 4 * P], U8, tag="scl", name="scl", align_bytes=64)
             nc.vector.quantize_mx(
                 out=codes[:].bitcast(FP8X4), scales=scl[:],
-                in_=st["grp", h, b][:].rearrange("p g q t -> p (g q t)"),
+                in_=st["grp", h, b // 2][:].rearrange("p g q t -> p (g q t)"),
             )
-            for i, (half, s) in enumerate(SET_BANKS[b]):
+            for i, (half, s) in enumerate(SET_BANKS[b - 1] + SET_BANKS[b]):
                 st["codes", h, half, s] = (codes, scl, slice(i * P, (i + 1) * P))
 
         def store(h, half):
-            rinv = gsmall.tile([P, GT], F32, tag="rinv", name="rinv")
-            nc.vector.reciprocal(out=rinv[:], in_=st["rs", h, half][:])
+            if half:
+                st["rinv", h] = gsmall.tile([P, 2, GT], F32, tag="rinv", name="rinv")
+                nc.vector.reciprocal(out=st["rinv", h][:], in_=st["rs", h][:])
+            rinv = st["rinv", h][:, half, :]
             ost = opool.tile([P, GT, P], F32, tag="ost", name="ost")
             nc.vector.tensor_tensor(
-                out=ost[:], in0=st["ob", h, half][:], in1=rinv[:].unsqueeze(2).to_broadcast([P, GT, P]),
+                out=ost[:], in0=st["ob", h, half][:], in1=rinv.unsqueeze(2).to_broadcast([P, GT, P]),
                 op=ALU.mult,
             )
             nc.sync.dma_start(
@@ -369,35 +375,31 @@ def tile_flexattention_kernel(tc, qkv, out):
 
         def exp(h, tile):
             half, j = int(tile[0] == "m"), int(tile[1])
-            if ("rs", h, half) not in st:
-                st["rs", h, half] = gsmall.tile([P, GT], F32, tag="rs%d" % half, name="rs")
+            if ("rs", h) not in st:
+                st["rs", h] = gsmall.tile([P, 2, GT], F32, tag="rs", name="rs")
             n = 5 if half else j + 1
             nc.scalar.activation(
                 out=es[half][h % N_E][:, :, SLOTS[tile] : SLOTS[tile] + n, :],
                 in_=st["z", h, tile][:, 0 : n * P].rearrange("p (b u w) -> p u b w", u=2, w=64),
                 func=ACT.Exp, bias=st["nbias", h, tile][:], scale=-1.0,
-                accum_out=st["rs", h, half][:, j : j + 1],
+                accum_out=st["rs", h][:, half, j : j + 1],
             )
 
         def e_copy(h, b):
-            grp = gpool.tile([P, 2, P, 4], BF16, tag="grp", name="grp", align_bytes=64)
-            nc.scalar.copy(
-                out=grp[:].rearrange("p c q t -> p (c q t)").bitcast(F32).rearrange("p (c q u) -> p c q u", c=2, u=2),
-                in_=st["bank", h, b][:].rearrange("p u c q -> p c q u"),
-            )
-            st["grp", h, b] = grp
+            if b % 2 == 0:
+                st["grp", h, b // 2] = gpool.tile([P, 4, P, 4], BF16, tag="grp", name="grp", align_bytes=64)
+            grp = st["grp", h, b // 2]
+            words = grp[:].rearrange("p c q t -> p (c q t)").bitcast(F32).rearrange("p (c q u) -> p c q u", c=4, u=2)
+            i = 2 * (b % 2)
+            nc.scalar.copy(out=words[:, i : i + 2], in_=st["bank", h, b][:].rearrange("p u c q -> p c q u"))
 
         def qk_copy(h, half):
-            qk_ps = st["qk_ps", h, half]
-            q_t = qpool.tile([P, GT, P], BF16, tag="q_t", name="q_t")
-            nc.scalar.copy(out=q_t[:].bitcast(F32), in_=qk_ps[:, 0:GT, :].bitcast(F32))
             if half == 0:
-                st["k_t", h] = kpool.tile([P, NQB, P], BF16, tag="k_t", name="k_t")
+                st["qk_t", h] = kpool.tile([P, 4 * GT, P], BF16, tag="qk_t", name="qk_t")
             nc.scalar.copy(
-                out=st["k_t", h][:, GT * half : GT * half + GT, :].bitcast(F32),
-                in_=qk_ps[:, GT : 2 * GT, :].bitcast(F32),
+                out=st["qk_t", h][:, 2 * GT * half : 2 * GT * (half + 1), :].bitcast(F32),
+                in_=st["qk_ps", h, half][:].bitcast(F32),
             )
-            st["q_t", h, half] = q_t
 
         def score_banks(k):
             h, p = divmod(k, 4)
@@ -421,14 +423,17 @@ def tile_flexattention_kernel(tc, qkv, out):
         for k in range(AT_BIAS, 4 * H + AT_MX[0] + 2):
             if set_bank_at(k):
                 e_transpose(*set_bank_at(k))
-            for half in range(2):
-                h = head_at(k, AT_QKT[half])
-                if h is not None:
+            qk_at_k = [(h, half) for half in range(2) for h in (head_at(k, AT_QKT[half]),) if h is not None]
+            if k >= 0:
+                for h, half in qk_at_k:
                     qk_transpose(h, half)
             for h, bank in score_banks(k):
                 masks(h, bank)
             for h, bank in score_banks(k):
                 scores(h, bank)
+            if k < 0:
+                for h, half in qk_at_k:
+                    qk_transpose(h, half)
             for half in (1, 0):
                 h = head_at(k, AT_MX[half])
                 if h is not None:
@@ -436,10 +441,8 @@ def tile_flexattention_kernel(tc, qkv, out):
             h = head_at(k, AT_BIAS)
             if h:
                 h_bias(h)
-            if k == 1:
-                zero_variants(1, nc.gpsimd)
-            if k == AT_QKT[1]:
-                zero_variants(0, nc.vector)
+            if k in (-1, 3):
+                zero_variants((k + 1) // 4)
             for h, bank in score_banks(k - LAG_PASS):
                 score_pass(h, bank)
             if set_bank_at(k - LAG_Q):
@@ -455,10 +458,8 @@ def tile_flexattention_kernel(tc, qkv, out):
                     exp((k - LAG_EXP) // 4, tile)
             if set_bank_at(k):
                 e_copy(*set_bank_at(k))
-            for half in range(2):
-                h = head_at(k, AT_QKT[half])
-                if h is not None:
-                    qk_copy(h, half)
+            for h, half in qk_at_k:
+                qk_copy(h, half)
             hg, r = divmod(k + 12, 16)
             if 1 <= hg < NHG and r < 4:
                 if r < 2:

@@ -31,17 +31,17 @@ SCORE_BANKS = (
     (("m2", 0), ("m3", 0)),
     (("q2q0", 0), ("window", 1)),
 )
-EXPS = (("m0", "m1"), ("q3", "q1"), ("m2", "m3"), ("q2", "q0"))
+EXPS = (("m0", "m1"), ("q3", "q1"), ("m2", "m3"), ("q0", "q2"))
 SLOTS = {"q1": 0, "q2": 4, "q0": 7, "q3": 8, "m0": 0, "m1": 5, "m2": 10, "m3": 15}
 SET_BANKS = (((1, 0), (1, 1)), ((0, 2), (0, 0)), ((1, 2), (1, 3)), ((1, 4), (0, 1)))
 AT_QKT = (-5, -3)
 AT_BIAS = -6
 LAG_PASS, LAG_EXP = 1, 2
 AT_TR = 3
-LAG_Q = 1
-AT_MX = (10, 8)
-V_FIRST = ((0, 1), (2, 3))
-V_NEXT = ((10, 14), (14, 18))
+LAG_Q = 2
+AT_MX = (12, 10)
+V_FIRST = (((0, 0, 0, 0), 4), ((1, 1, 1, 1), 5))
+V_NEXT = (((9, 10, 11, 12), 14), ((13, 14, 15, 16), 18))
 N_E = 3
 
 
@@ -196,13 +196,15 @@ def tile_flexattention_kernel(tc, qkv, out):
                 nc.gpsimd.memset(vvar[i][key][:], 0)
             nc.gpsimd.memset(vmscales[i][:].bitcast(U32), 0)
 
-        def v_copy(hg, c):
-            gv = vpool.tile([P, GH * E, 4], BF16, tag="gv", name="gv", align_bytes=64)
-            nc.vector.tensor_copy(
-                out=gv[:].rearrange("p (c i) t -> p c t i", i=4),
-                in_=st["vraw", hg][:, c].rearrange("p t (c i) -> p c t i", i=4),
+        def v_copy(hg, c, i):
+            if i == 0:
+                st["gv", hg, c] = vpool.tile([P, GH * E, 4], BF16, tag="gv", name="gv", align_bytes=64)
+            cols = slice(i * E, (i + 1) * E)
+            nc.gpsimd.tensor_scalar(
+                out=st["gv", hg, c][:, cols, :],
+                in0=st["vraw", hg][:, c, :, cols].rearrange("p t x -> p x t"),
+                scalar1=1.0, scalar2=0.0, op0=ALU.mult, op1=ALU.add,
             )
-            st["gv", hg, c] = gv
 
         def v_quantise(hg, c):
             codes = vpool.tile([P, GH * E], U32, tag="vcodes%d" % c, name="vcodes", align_bytes=64)
@@ -417,7 +419,8 @@ def tile_flexattention_kernel(tc, qkv, out):
         for hg in range(NHG):
             for c in range(2):
                 base, (at_copy, at_q) = (0, V_FIRST[c]) if hg == 0 else (16 * (hg - 1), V_NEXT[c])
-                v_plan.setdefault(base + at_copy, []).append((v_copy, hg, c))
+                for i in range(4):
+                    v_plan.setdefault(base + at_copy[i], []).append((v_copy, hg, c, i))
                 v_plan.setdefault(base + at_q, []).append((v_quantise, hg, c))
 
         for k in range(AT_BIAS, 4 * H + AT_MX[0] + 2):
@@ -443,16 +446,16 @@ def tile_flexattention_kernel(tc, qkv, out):
                 h_bias(h)
             if k in (-1, 3):
                 zero_variants((k + 1) // 4)
-            for h, bank in score_banks(k - LAG_PASS):
-                score_pass(h, bank)
             if set_bank_at(k - LAG_Q):
                 quantise(*set_bank_at(k - LAG_Q))
+            for h, bank in reversed(score_banks(k - LAG_PASS)):
+                score_pass(h, bank)
             for half in (1, 0):
                 h = head_at(k, AT_MX[half] + 1)
                 if h is not None:
                     store(h, half)
-            for stage, hg, c in v_plan.get(k, []):
-                stage(hg, c)
+            for stage, *index in v_plan.get(k, []):
+                stage(*index)
             if 0 <= k - LAG_EXP < 4 * H:
                 for tile in EXPS[(k - LAG_EXP) % 4]:
                     exp((k - LAG_EXP) // 4, tile)

@@ -179,7 +179,7 @@ def tile_flexattention_kernel(tc, qkv, out):
             [const.tile([P, 2, 20, 64], BF16, name="eb%d" % i) for i in range(N_E)],
         )
         for e in es[0]:
-            nc.gpsimd.memset(e[:, :, 2:4, :], 0.0)
+            nc.vector.memset(e[:, :, 2:4, :], 0.0)
         VARIANTS = {
             ("hi", 1): (0, 32, 128), ("hi", 2): (0, 64, 128), ("hi", 3): (0, 96, 128),
             ("lo", 0): (1, 0, 32), ("lo", 1): (1, 0, 64), ("lo", 2): (1, 0, 96),
@@ -191,10 +191,21 @@ def tile_flexattention_kernel(tc, qkv, out):
         ]
         vmscales = [const.tile([P, GH * E], U8, name="vms%d" % i, align_bytes=64) for i in range(2)]
 
+        zeros = const.tile([P, GH * E], U32, name="zeros")
+        nc.vector.memset(zeros[:], 0)
+        for scl in vmscales:
+            nc.vector.memset(scl[:].bitcast(U32), 0)
+
+        def live(key):
+            return (96, 128) if key[0] == "moved" else VARIANTS[key][1:]
+
         def zero_variants(i):
             for key in VARIANTS:
-                nc.gpsimd.memset(vvar[i][key][:], 0)
-            nc.gpsimd.memset(vmscales[i][:].bitcast(U32), 0)
+                for p0, p1 in ((0, live(key)[0]), (live(key)[1], P)):
+                    if p0 < p1:
+                        nc.sync.dma_start(
+                            out=vvar[i][key][p0:p1, :].bitcast(I32), in_=zeros[p0:p1, :].bitcast(I32)
+                        )
 
         def v_copy(hg, c, i):
             if i == 0:
@@ -216,7 +227,7 @@ def tile_flexattention_kernel(tc, qkv, out):
             st["v", hg, c] = (codes, scl)
             for key, (half, p0, p1) in VARIANTS.items():
                 if half == c:
-                    q0, q1 = (96, 128) if key[0] == "moved" else (p0, p1)
+                    q0, q1 = live(key)
                     nc.sync.dma_start(
                         out=vvar[hg % 2][key][q0:q1, :].bitcast(I32), in_=codes[p0:p1, :].bitcast(I32)
                     )
@@ -444,8 +455,8 @@ def tile_flexattention_kernel(tc, qkv, out):
             h = head_at(k, AT_BIAS)
             if h:
                 h_bias(h)
-            if k in (-1, 3):
-                zero_variants((k + 1) // 4)
+            if k in (-1, 7):
+                zero_variants((k + 1) // 8)
             if set_bank_at(k - LAG_Q):
                 quantise(*set_bank_at(k - LAG_Q))
             for h, bank in reversed(score_banks(k - LAG_PASS)):

@@ -35,7 +35,7 @@ EXPS = (("m0", "m1"), ("q3", "q1"), ("m2", "m3"), ("q0", "q2"))
 SLOTS = {"q1": 0, "q2": 4, "q0": 7, "q3": 8, "m0": 0, "m1": 5, "m2": 10, "m3": 15}
 SET_BANKS = (((1, 0), (1, 1)), ((0, 2), (0, 0)), ((1, 2), (1, 3)), ((1, 4), (0, 1)))
 AT_QKT = (-5, -3)
-AT_BIAS = -6
+AT_BIAS = -10
 LAG_PASS, LAG_EXP = 1, 2
 AT_TR = 3
 LAG_Q = 2
@@ -55,7 +55,7 @@ def tile_flexattention_kernel(tc, qkv, out):
         ctx.enter_context(tc.manual_schedule())
         const = ctx.enter_context(tc.tile_pool(name="const", bufs=1))
         ld = ctx.enter_context(tc.tile_pool(name="ld", bufs=2))
-        bpool = ctx.enter_context(tc.tile_pool(name="bpool", bufs=4))
+        bpool = ctx.enter_context(tc.tile_pool(name="bpool", bufs=5))
         kpool = ctx.enter_context(tc.tile_pool(name="kpool", bufs=4))
         vpool = ctx.enter_context(tc.tile_pool(name="vpool", bufs=2))
         small = ctx.enter_context(tc.tile_pool(name="small", bufs=16))
@@ -94,6 +94,9 @@ def tile_flexattention_kernel(tc, qkv, out):
         load_qk(0, 1, 1, GH)
         load_v(0, 0)
         load_v(0, 1)
+        for i in range(2):
+            load_qk(1, i)
+            load_v(1, i)
 
         ident_bf = const.tile([P, P], BF16, name="ident_bf")
         make_identity(nc, ident_bf[:])
@@ -109,6 +112,23 @@ def tile_flexattention_kernel(tc, qkv, out):
             out=perm_f[:].rearrange("p (u r w) -> p u r w", u=2, w=2),
             in_=ident_f[:].rearrange("p (r u w) -> p u r w", u=2, w=2),
         )
+        part_t = const.tile([P, 1], F32, name="part_t")
+        for p0 in range(0, P, 32):
+            nc.gpsimd.iota(
+                part_t[p0 : p0 + 32, :], pattern=[[0, 1]], base=0, channel_multiplier=1,
+                allow_small_or_imprecise_dtypes=True,
+            )
+        offset_t = const.tile([P, 3, P], BF16, name="offset_t")
+        nc.gpsimd.iota(
+            offset_t[:].rearrange("p b (u r w) -> p b u r w", u=2, w=2),
+            pattern=[[0, 3], [2, 2], [4, 32], [1, 2]], base=0, channel_multiplier=0,
+            allow_small_or_imprecise_dtypes=True,
+        )
+        block_t = const.tile([P, 3, P], BF16, name="block_t")
+        nc.gpsimd.iota(
+            block_t[:], pattern=[[P, 3], [0, P]], base=-3 * P, channel_multiplier=0,
+            allow_small_or_imprecise_dtypes=True,
+        )
         key_t = const.tile([P, 2, P], F32, name="key_t")
         nc.gpsimd.iota(
             key_t[:], pattern=[[-512, 2], [0, P]], base=0, channel_multiplier=1,
@@ -121,18 +141,6 @@ def tile_flexattention_kernel(tc, qkv, out):
         nc.gpsimd.affine_select(
             out=key_t[:, 1, :], in_=key_t[:, 1, :], pattern=[[-1, P]],
             compare_op=ALU.is_gt, fill=-MASKED, base=0, channel_multiplier=1,
-        )
-        part_i = const.tile([P, 1], I32, name="part_i")
-        nc.gpsimd.iota(part_i[:], pattern=[[0, 1]], base=0, channel_multiplier=1)
-        heads_t = const.tile([P, H], F32, name="heads_t")
-        nc.gpsimd.iota(
-            heads_t[:], pattern=[[1, H]], base=0, channel_multiplier=0, allow_small_or_imprecise_dtypes=True
-        )
-        far_t = const.tile([P, 3, P], F32, name="far_t")
-        nc.gpsimd.iota(
-            far_t[:].rearrange("p b (u r w) -> p b u r w", u=2, w=2),
-            pattern=[[P, 3], [2, 2], [4, 32], [1, 2]], base=-3 * P, channel_multiplier=0,
-            allow_small_or_imprecise_dtypes=True,
         )
 
         def h_bias(h):
@@ -147,39 +155,42 @@ def tile_flexattention_kernel(tc, qkv, out):
                 )
             st["bias", h] = bias_t
 
-        h_bias(0)
-        nc.vector.tensor_scalar(out=part_i[:], in0=part_i[:], scalar1=31, scalar2=None, op0=ALU.bitwise_and)
-        part_f = const.tile([P, 1], F32, name="part_f")
-        nc.vector.tensor_copy(out=part_f[:], in_=part_i[:])
-        pick = const.tile([P, H], BF16, name="pick")
-        nc.vector.tensor_scalar(out=pick[:], in0=heads_t[:], scalar1=part_f[:], scalar2=None, op0=ALU.is_equal)
+        first_t = const.tile([P, 1], F32, name="first_t")
+        second_t = const.tile([P, 1], F32, name="second_t")
         sigmas = const.tile([P, H], F32, name="sigmas")
-        for h in range(H):
+        slopes = const.tile([P, H], BF16, name="slopes")
+        mid = const.tile([P, H], BF16, name="mid")
+        part_places = const.tile([P, 3 * P], BF16, name="part_places")
+        places = const.tile([P, 3 * P], BF16, name="places")
+        for h in range(2):
             nc.vector.tensor_scalar(
-                out=sigmas[:, h : h + 1], in0=part_f[:], scalar1=float(h), scalar2=sigma_of(h),
-                op0=ALU.is_equal, op1=ALU.mult,
+                out=sigmas[:, h : h + 1], in0=part_t[:], scalar1=0.0, scalar2=sigma_of(h), op0=ALU.mult, op1=ALU.add
             )
-        sigma = const.tile([P, 1], F32, name="sigma")
-        nc.vector.reduce_sum(out=sigma[:], in_=sigmas[:], axis=mybir.AxisListType.X)
-        rest = const.tile([P, 3 * P], F32, name="rest")
-        alibi = const.tile([P, 3 * P], BF16, name="alibi")
-        mid = const.tile([P, 3 * P], BF16, name="mid")
+        nc.vector.tensor_scalar(out=first_t[:], in0=part_t[:], scalar1=0.0, scalar2=None, op0=ALU.is_equal)
+        nc.vector.tensor_scalar(out=second_t[:], in0=part_t[:], scalar1=1.0, scalar2=None, op0=ALU.is_equal)
+        nc.vector.tensor_scalar(out=sigmas[:, 2:4], in0=sigmas[:, 0:2], scalar1=0.5, scalar2=None, op0=ALU.mult)
         nc.vector.tensor_scalar(
-            out=rest[:], in0=far_t[:].rearrange("p b c -> p (b c)"), scalar1=sigma[:], scalar2=None, op0=ALU.mult
+            out=part_places[:], in0=offset_t[:].rearrange("p b c -> p (b c)"), scalar1=first_t[:], scalar2=None,
+            op0=ALU.mult,
         )
-        nc.vector.tensor_copy(out=alibi[:], in_=rest[:])
-        nc.vector.tensor_tensor(out=rest[:], in0=rest[:], in1=alibi[:], op=ALU.subtract)
-        nc.vector.tensor_copy(out=mid[:], in_=rest[:])
-        nc.vector.tensor_tensor(out=rest[:], in0=rest[:], in1=mid[:], op=ALU.subtract)
-        nc.vector.tensor_copy(out=alibi[32:64, :], in_=mid[32:64, :])
-        nc.vector.tensor_copy(out=alibi[64:96, :], in_=rest[64:96, :])
-        nc.vector.memset(alibi[96:128, :], 0.0)
+        nc.vector.tensor_scalar(out=sigmas[:, 4:8], in0=sigmas[:, 0:4], scalar1=0.25, scalar2=None, op0=ALU.mult)
+        nc.vector.scalar_tensor_tensor(
+            out=places[:], in0=block_t[:].rearrange("p b c -> p (b c)"), scalar=second_t[:], in1=part_places[:],
+            op0=ALU.mult, op1=ALU.add,
+        )
+        nc.vector.tensor_scalar(out=sigmas[:, 8:16], in0=sigmas[:, 0:8], scalar1=0.0625, scalar2=None, op0=ALU.mult)
+        h_bias(0)
+        nc.vector.tensor_copy(out=slopes[:], in_=sigmas[:])
+        nc.vector.tensor_tensor(out=sigmas[:], in0=sigmas[:], in1=slopes[:], op=ALU.subtract)
+        nc.vector.tensor_copy(out=mid[:], in_=sigmas[:])
+        nc.vector.tensor_copy(out=slopes[32:64, :], in_=mid[32:64, :])
+        nc.vector.tensor_tensor(out=sigmas[:], in0=sigmas[:], in1=mid[:], op=ALU.subtract)
+        nc.vector.tensor_copy(out=slopes[64:96, :], in_=sigmas[64:96, :])
+        nc.vector.memset(slopes[96:128, :], 0.0)
         es = (
             [const.tile([P, 2, 12, 64], BF16, name="ea%d" % i) for i in range(N_E)],
             [const.tile([P, 2, 20, 64], BF16, name="eb%d" % i) for i in range(N_E)],
         )
-        for e in es[0]:
-            nc.vector.memset(e[:, :, 2:4, :], 0.0)
         VARIANTS = {
             ("hi", 1): (0, 32, 128), ("hi", 2): (0, 64, 128), ("hi", 3): (0, 96, 128),
             ("lo", 0): (1, 0, 32), ("lo", 1): (1, 0, 64), ("lo", 2): (1, 0, 96),
@@ -192,9 +203,13 @@ def tile_flexattention_kernel(tc, qkv, out):
         vmscales = [const.tile([P, GH * E], U8, name="vms%d" % i, align_bytes=64) for i in range(2)]
 
         zeros = const.tile([P, GH * E], U32, name="zeros")
-        nc.vector.memset(zeros[:], 0)
-        for scl in vmscales:
-            nc.vector.memset(scl[:].bitcast(U32), 0)
+
+        def zero_tiles():
+            nc.vector.memset(zeros[:], 0)
+            for scl in vmscales:
+                nc.vector.memset(scl[:].bitcast(U32), 0)
+            for e in es[0]:
+                nc.vector.memset(e[:, :, 2:4, :], 0.0)
 
         def live(key):
             return (96, 128) if key[0] == "moved" else VARIANTS[key][1:]
@@ -282,8 +297,8 @@ def tile_flexattention_kernel(tc, qkv, out):
 
             def far(n):
                 nc.tensor.matmul(
-                    sb[:, 0 : n * P], lhsT=pick[:, h : h + 1].to_broadcast([P, P]),
-                    rhs=alibi[:, (3 - n) * P : 3 * P], start=False, stop=False,
+                    sb[:, 0 : n * P], lhsT=slopes[:, h : h + 1].to_broadcast([P, P]),
+                    rhs=places[:, (3 - n) * P : 3 * P], start=False, stop=False,
                 )
 
             if bank == "window":
@@ -455,12 +470,14 @@ def tile_flexattention_kernel(tc, qkv, out):
             h = head_at(k, AT_BIAS)
             if h:
                 h_bias(h)
-            if k in (-1, 7):
-                zero_variants((k + 1) // 8)
             if set_bank_at(k - LAG_Q):
                 quantise(*set_bank_at(k - LAG_Q))
             for h, bank in reversed(score_banks(k - LAG_PASS)):
                 score_pass(h, bank)
+            if k == 2:
+                zero_tiles()
+                zero_variants(0)
+                zero_variants(1)
             for half in (1, 0):
                 h = head_at(k, AT_MX[half] + 1)
                 if h is not None:
@@ -474,9 +491,7 @@ def tile_flexattention_kernel(tc, qkv, out):
                 e_copy(*set_bank_at(k))
             for h, half in qk_at_k:
                 qk_copy(h, half)
-            hg, r = divmod(k + 12, 16)
-            if 1 <= hg < NHG and r < 4:
-                if r < 2:
-                    load_qk(hg, r)
-                else:
-                    load_v(hg, r - 2)
+            hg, r = divmod(k + 22, 16)
+            if 2 <= hg < NHG and r < 2:
+                load_qk(hg, r)
+                load_v(hg, r)

@@ -31,18 +31,19 @@ SCORE_BANKS = (
     (("m2", 0), ("m3", 0)),
     (("q2q0", 0), ("window", 1)),
 )
-EXPS = (("m0", "m1"), ("q3", "q1"), ("m2", "m3"), ("q0", "q2"))
+EXPS = (("m0", "m1"), ("q3", "q1"), ("m2", "m3"), ("q2", "q0"))
 SLOTS = {"q1": 0, "q2": 4, "q0": 7, "q3": 8, "m0": 0, "m1": 5, "m2": 10, "m3": 15}
 SET_BANKS = (((1, 0), (1, 1)), ((0, 2), (0, 0)), ((1, 2), (1, 3)), ((1, 4), (0, 1)))
 AT_QKT = (-5, -3)
 AT_BIAS = -10
 LAG_PASS, LAG_EXP = 1, 2
 AT_TR = 3
-LAG_Q = 2
-AT_MX = (12, 10)
+LAG_Q = 1
+AT_MX = (11, 9)
 V_FIRST = (((0, 0, 0, 0), 4), ((1, 1, 1, 1), 5))
 V_NEXT = (((9, 10, 11, 12), 14), ((13, 14, 15, 16), 18))
 N_E = 3
+N_WARM = 5
 
 
 def sigma_of(h):
@@ -97,6 +98,12 @@ def tile_flexattention_kernel(tc, qkv, out):
         for i in range(2):
             load_qk(1, i)
             load_v(1, i)
+
+        warm = const.tile([P, 4 * P], BF16, name="warm")
+        nc.vector.memset(warm[:], 0.0)
+        warm_ps = ps_s.tile([P, 4 * P], F32, tag="s", name="warm_ps")
+        for i in range(N_WARM):
+            nc.tensor.matmul(warm_ps[:], lhsT=warm[:, 0:P], rhs=warm[:], start=(i == 0), stop=(i == N_WARM - 1))
 
         ident_bf = const.tile([P, P], BF16, name="ident_bf")
         make_identity(nc, ident_bf[:])
@@ -470,13 +477,14 @@ def tile_flexattention_kernel(tc, qkv, out):
             h = head_at(k, AT_BIAS)
             if h:
                 h_bias(h)
+            for h, bank in score_banks(k - LAG_PASS):
+                score_pass(h, bank)
             if set_bank_at(k - LAG_Q):
                 quantise(*set_bank_at(k - LAG_Q))
-            for h, bank in reversed(score_banks(k - LAG_PASS)):
-                score_pass(h, bank)
             if k == 2:
                 zero_tiles()
                 zero_variants(0)
+            if k == 6:
                 zero_variants(1)
             for half in (1, 0):
                 h = head_at(k, AT_MX[half] + 1)

@@ -448,6 +448,12 @@ def tile_flexattention_kernel(tc, qkv, out):
             h, b = divmod(k - AT_TR, 4)
             return (h, b) if 0 <= h < H else None
 
+        def mx_at(k):
+            for half in (1, 0):
+                h = head_at(k, AT_MX[half])
+                if h is not None:
+                    mx(h, half)
+
         v_plan = {}
         for hg in range(NHG):
             for c in range(2):
@@ -465,15 +471,15 @@ def tile_flexattention_kernel(tc, qkv, out):
                     qk_transpose(h, half)
             for h, bank in score_banks(k):
                 masks(h, bank)
-            for h, bank in score_banks(k):
+            for i, (h, bank) in enumerate(score_banks(k)):
+                if i == 1:
+                    mx_at(k)
                 scores(h, bank)
+            if len(score_banks(k)) < 2:
+                mx_at(k)
             if k < 0:
                 for h, half in qk_at_k:
                     qk_transpose(h, half)
-            for half in (1, 0):
-                h = head_at(k, AT_MX[half])
-                if h is not None:
-                    mx(h, half)
             h = head_at(k, AT_BIAS)
             if h:
                 h_bias(h)

@@ -40,6 +40,7 @@ LAG_PASS, LAG_EXP = 1, 2
 AT_TR = 3
 LAG_Q = 1
 AT_MX = (11, 9)
+AT_RINV = 6
 V_FIRST = (((0, 0, 0, 0), 4), ((1, 1, 1, 1), 5))
 V_NEXT = (((9, 10, 11, 12), 14), ((13, 14, 15, 16), 18))
 N_E = 3
@@ -394,10 +395,11 @@ def tile_flexattention_kernel(tc, qkv, out):
             for i, (half, s) in enumerate(SET_BANKS[b - 1] + SET_BANKS[b]):
                 st["codes", h, half, s] = (codes, scl, slice(i * P, (i + 1) * P))
 
+        def reciprocals(h):
+            st["rinv", h] = gsmall.tile([P, 2, GT], F32, tag="rinv", name="rinv")
+            nc.vector.reciprocal(out=st["rinv", h][:], in_=st["rs", h][:])
+
         def store(h, half):
-            if half:
-                st["rinv", h] = gsmall.tile([P, 2, GT], F32, tag="rinv", name="rinv")
-                nc.vector.reciprocal(out=st["rinv", h][:], in_=st["rs", h][:])
             rinv = st["rinv", h][:, half, :]
             ost = opool.tile([P, GT, P], F32, tag="ost", name="ost")
             nc.vector.tensor_tensor(
@@ -487,6 +489,9 @@ def tile_flexattention_kernel(tc, qkv, out):
                 score_pass(h, bank)
             if set_bank_at(k - LAG_Q):
                 quantise(*set_bank_at(k - LAG_Q))
+            h = head_at(k, AT_RINV)
+            if h is not None:
+                reciprocals(h)
             if k == 2:
                 zero_tiles()
                 zero_variants(0)

@@ -34,7 +34,7 @@ SCORE_BANKS = (
 EXPS = (("m0", "m1"), ("q3", "q1"), ("m2", "m3"), ("q2", "q0"))
 SLOTS = {"q1": 0, "q2": 4, "q0": 7, "q3": 8, "m0": 0, "m1": 5, "m2": 10, "m3": 15}
 SET_BANKS = (((1, 0), (1, 1)), ((0, 2), (0, 0)), ((1, 2), (1, 3)), ((1, 4), (0, 1)))
-AT_QKT = (-5, -3)
+AT_QKT = (-4, -2)
 AT_BIAS = -10
 LAG_PASS, LAG_EXP = 1, 2
 AT_TR = 3
@@ -468,7 +468,7 @@ def tile_flexattention_kernel(tc, qkv, out):
             if set_bank_at(k):
                 e_transpose(*set_bank_at(k))
             qk_at_k = [(h, half) for half in range(2) for h in (head_at(k, AT_QKT[half]),) if h is not None]
-            if k >= 0:
+            if k > 0:
                 for h, half in qk_at_k:
                     qk_transpose(h, half)
             for h, bank in score_banks(k):
@@ -479,7 +479,7 @@ def tile_flexattention_kernel(tc, qkv, out):
                 scores(h, bank)
             if len(score_banks(k)) < 2:
                 mx_at(k)
-            if k < 0:
+            if k <= 0:
                 for h, half in qk_at_k:
                     qk_transpose(h, half)
             h = head_at(k, AT_BIAS)

@@ -384,15 +384,20 @@ def tile_flexattention_kernel(tc, qkv, out):
                 st["nbias", h, tile] = nbias
 
         def quantise(h, b):
-            if b % 2 == 0:
+            if h == H - 1:
+                first, banks = 2 * (b % 2), SET_BANKS[b]
+            elif b % 2 == 0:
                 return
+            else:
+                first, banks = 0, SET_BANKS[b - 1] + SET_BANKS[b]
+            n = len(banks)
             codes = cpool.tile([P, 4 * P], U32, tag="codes", name="codes", align_bytes=64)
             scl = cpool.tile([P, 4 * P], U8, tag="scl", name="scl", align_bytes=64)
             nc.vector.quantize_mx(
-                out=codes[:].bitcast(FP8X4), scales=scl[:],
-                in_=st["grp", h, b // 2][:].rearrange("p g q t -> p (g q t)"),
+                out=codes[:, 0 : n * P].bitcast(FP8X4), scales=scl[:, 0 : n * P],
+                in_=st["grp", h, b // 2][:, first : first + n].rearrange("p g q t -> p (g q t)"),
             )
-            for i, (half, s) in enumerate(SET_BANKS[b - 1] + SET_BANKS[b]):
+            for i, (half, s) in enumerate(banks):
                 st["codes", h, half, s] = (codes, scl, slice(i * P, (i + 1) * P))
 
         def reciprocals(h):
@@ -468,14 +473,14 @@ def tile_flexattention_kernel(tc, qkv, out):
             if set_bank_at(k):
                 e_transpose(*set_bank_at(k))
             qk_at_k = [(h, half) for half in range(2) for h in (head_at(k, AT_QKT[half]),) if h is not None]
-            if k > 0:
-                for h, half in qk_at_k:
-                    qk_transpose(h, half)
             for h, bank in score_banks(k):
                 masks(h, bank)
             for i, (h, bank) in enumerate(score_banks(k)):
                 if i == 1:
                     mx_at(k)
+                    if k > 0:
+                        for hq, half in qk_at_k:
+                            qk_transpose(hq, half)
                 scores(h, bank)
             if len(score_banks(k)) < 2:
                 mx_at(k)

from contextlib import ExitStack
import math

import concourse.mybir as mybir
from concourse.masks import make_identity

F32 = mybir.dt.float32
BF16 = mybir.dt.bfloat16
I32 = mybir.dt.int32
U32 = mybir.dt.uint32
U8 = mybir.dt.uint8
FP8X4 = mybir.dt.float8_e4m3fn_x4
ALU = mybir.AluOpType
ACT = mybir.ActivationFunctionType

P = 128
H = 16
L = 1024
E = 128
NQB = L // P
GH = 4
NHG = H // GH
GT = 4
SCALE = 1.0 / math.sqrt(E)
MASKED = 1.0e30
FLOPS = 4 * E * H * (512 * 512 + 512 * 1024)

SCORE_BANKS = (
    (("m0", 0), ("m1", 0)),
    (("q3", 0), ("q1", 0)),
    (("m2", 0), ("m3", 0)),
    (("q2q0", 0), ("window", 1)),
)
EXPS = (("m0", "m1"), ("q3", "q1"), ("m2", "m3"), ("q2", "q0"))
SLOTS = {"q1": 0, "q2": 4, "q0": 7, "q3": 8, "m0": 0, "m1": 5, "m2": 10, "m3": 15}
SET_BANKS = (((1, 0), (1, 1)), ((0, 2), (0, 0)), ((1, 2), (1, 3)), ((1, 4), (0, 1)))
AT_QKT = (-4, -2)
AT_BIAS = -10
LAG_PASS, LAG_EXP = 1, 2
AT_TR = 3
LAG_Q = 1
AT_MX = (11, 9)
AT_RINV = 6
V_FIRST = (((0, 0, 0, 0), 4), ((1, 1, 1, 1), 5))
V_NEXT = (((9, 10, 11, 12), 14), ((13, 14, 15, 16), 18))
N_E = 3
N_WARM = 5


def sigma_of(h):
    return 2.0 ** (-(h + 1) / 2.0) * math.sqrt(E)


def tile_flexattention_kernel(tc, qkv, out):
    nc = tc.nc
    with ExitStack() as ctx:
        ctx.enter_context(tc.manual_schedule())
        const = ctx.enter_context(tc.tile_pool(name="const", bufs=1))
        ld = ctx.enter_context(tc.tile_pool(name="ld", bufs=2))
        bpool = ctx.enter_context(tc.tile_pool(name="bpool", bufs=5))
        kpool = ctx.enter_context(tc.tile_pool(name="kpool", bufs=4))
        vpool = ctx.enter_context(tc.tile_pool(name="vpool", bufs=2))
        small = ctx.enter_context(tc.tile_pool(name="small", bufs=16))
        gsmall = ctx.enter_context(tc.tile_pool(name="gsmall", bufs=8))
        zpool = ctx.enter_context(tc.tile_pool(name="zpool", bufs=8))
        gpool = ctx.enter_context(tc.tile_pool(name="gpool", bufs=4))
        cpool = ctx.enter_context(tc.tile_pool(name="cpool", bufs=8))
        opool = ctx.enter_context(tc.tile_pool(name="opool", bufs=4))
        ps_s = ctx.enter_context(tc.psum_pool(name="ps_s", bufs=4))
        ps_t = ctx.enter_context(tc.psum_pool(name="ps_t", bufs=2))
        ps_a = ctx.enter_context(tc.psum_pool(name="ps_a", bufs=2))

        st = {}

        qksrc = qkv[0].rearrange("(b p) w h e -> p w b (h e)", p=P)
        vsrc = qkv[0, :, 2].rearrange("(c p t) h e -> p c t (h e)", p=P, t=4)

        def load_qk(hg, w, h0=0, h1=GH):
            if w == 0 and h0 == 0:
                st["x", hg] = ld.tile([P, 2, NQB, GH * E], BF16, tag="x", name="x")
            nc.sync.dma_start(
                out=st["x", hg][:, w, :, h0 * E : h1 * E],
                in_=qksrc[:, w, :, (hg * GH + h0) * E : (hg * GH + h1) * E],
            )

        def load_v(hg, c):
            if c == 0:
                st["vraw", hg] = ld.tile([P, 2, 4, GH * E], BF16, tag="vraw", name="vraw")
            nc.sync.dma_start(
                out=st["vraw", hg][:, c], in_=vsrc[:, c, :, hg * GH * E : (hg + 1) * GH * E]
            )

        load_qk(0, 0, 0, 1)
        load_qk(0, 1, 0, 1)
        load_qk(0, 0, 1, GH)
        load_qk(0, 1, 1, GH)
        load_v(0, 0)
        load_v(0, 1)
        for i in range(2):
            load_qk(1, i)
            load_v(1, i)

        warm = const.tile([P, 4 * P], BF16, name="warm")
        nc.vector.memset(warm[:], 0.0)
        warm_ps = ps_s.tile([P, 4 * P], F32, tag="s", name="warm_ps")
        for i in range(N_WARM):
            nc.tensor.matmul(warm_ps[:], lhsT=warm[:, 0:P], rhs=warm[:], start=(i == 0), stop=(i == N_WARM - 1))

        ident_bf = const.tile([P, P], BF16, name="ident_bf")
        make_identity(nc, ident_bf[:])
        perm_bf = const.tile([P, P], BF16, name="perm_bf")
        nc.vector.tensor_copy(
            out=perm_bf[:].rearrange("p (u r w) -> p u r w", u=2, w=2),
            in_=ident_bf[:].rearrange("p (r u w) -> p u r w", u=2, w=2),
        )
        ident_f = const.tile([P, P], F32, name="ident_f")
        make_identity(nc, ident_f[:])
        perm_f = const.tile([P, P], F32, name="perm_f")
        nc.vector.tensor_copy(
            out=perm_f[:].rearrange("p (u r w) -> p u r w", u=2, w=2),
            in_=ident_f[:].rearrange("p (r u w) -> p u r w", u=2, w=2),
        )
        part_t = const.tile([P, 1], F32, name="part_t")
        for p0 in range(0, P, 32):
            nc.gpsimd.iota(
                part_t[p0 : p0 + 32, :], pattern=[[0, 1]], base=0, channel_multiplier=1,
                allow_small_or_imprecise_dtypes=True,
            )
        offset_t = const.tile([P, 3, P], BF16, name="offset_t")
        nc.gpsimd.iota(
            offset_t[:].rearrange("p b (u r w) -> p b u r w", u=2, w=2),
            pattern=[[0, 3], [2, 2], [4, 32], [1, 2]], base=0, channel_multiplier=0,
            allow_small_or_imprecise_dtypes=True,
        )
        block_t = const.tile([P, 3, P], BF16, name="block_t")
        nc.gpsimd.iota(
            block_t[:], pattern=[[P, 3], [0, P]], base=-3 * P, channel_multiplier=0,
            allow_small_or_imprecise_dtypes=True,
        )
        key_t = const.tile([P, 2, P], F32, name="key_t")
        nc.gpsimd.iota(
            key_t[:], pattern=[[-512, 2], [0, P]], base=0, channel_multiplier=1,
            allow_small_or_imprecise_dtypes=True,
        )
        nc.gpsimd.affine_select(
            out=key_t[:, 0, :], in_=key_t[:, 0, :], pattern=[[1, P]],
            compare_op=ALU.is_ge, fill=-MASKED, base=0, channel_multiplier=-1,
        )
        nc.gpsimd.affine_select(
            out=key_t[:, 1, :], in_=key_t[:, 1, :], pattern=[[-1, P]],
            compare_op=ALU.is_gt, fill=-MASKED, base=0, channel_multiplier=1,
        )

        def h_bias(h):
            bias_t = bpool.tile([P, 2, P], F32, tag="bias", name="bias_t")
            if h:
                nc.gpsimd.tensor_scalar(
                    out=bias_t[:], in0=key_t[:], scalar1=sigma_of(h), scalar2=0.0, op0=ALU.mult, op1=ALU.add,
                )
            else:
                nc.vector.tensor_scalar(
                    out=bias_t[:], in0=key_t[:], scalar1=sigma_of(h), scalar2=None, op0=ALU.mult
                )
            st["bias", h] = bias_t

        first_t = const.tile([P, 1], F32, name="first_t")
        second_t = const.tile([P, 1], F32, name="second_t")
        sigmas = const.tile([P, H], F32, name="sigmas")
        slopes = const.tile([P, H], BF16, name="slopes")
        mid = const.tile([P, H], BF16, name="mid")
        part_places = const.tile([P, 3 * P], BF16, name="part_places")
        places = const.tile([P, 3 * P], BF16, name="places")
        for h in range(2):
            nc.vector.tensor_scalar(
                out=sigmas[:, h : h + 1], in0=part_t[:], scalar1=0.0, scalar2=sigma_of(h), op0=ALU.mult, op1=ALU.add
            )
        nc.vector.tensor_scalar(out=first_t[:], in0=part_t[:], scalar1=0.0, scalar2=None, op0=ALU.is_equal)
        nc.vector.tensor_scalar(out=second_t[:], in0=part_t[:], scalar1=1.0, scalar2=None, op0=ALU.is_equal)
        nc.vector.tensor_scalar(out=sigmas[:, 2:4], in0=sigmas[:, 0:2], scalar1=0.5, scalar2=None, op0=ALU.mult)
        nc.vector.tensor_scalar(
            out=part_places[:], in0=offset_t[:].rearrange("p b c -> p (b c)"), scalar1=first_t[:], scalar2=None,
            op0=ALU.mult,
        )
        nc.vector.tensor_scalar(out=sigmas[:, 4:8], in0=sigmas[:, 0:4], scalar1=0.25, scalar2=None, op0=ALU.mult)
        nc.vector.scalar_tensor_tensor(
            out=places[:], in0=block_t[:].rearrange("p b c -> p (b c)"), scalar=second_t[:], in1=part_places[:],
            op0=ALU.mult, op1=ALU.add,
        )
        nc.vector.tensor_scalar(out=sigmas[:, 8:16], in0=sigmas[:, 0:8], scalar1=0.0625, scalar2=None, op0=ALU.mult)
        h_bias(0)
        nc.vector.tensor_copy(out=slopes[:], in_=sigmas[:])
        nc.vector.tensor_tensor(out=sigmas[:], in0=sigmas[:], in1=slopes[:], op=ALU.subtract)
        nc.vector.tensor_copy(out=mid[:], in_=sigmas[:])
        nc.vector.tensor_copy(out=slopes[32:64, :], in_=mid[32:64, :])
        nc.vector.tensor_tensor(out=sigmas[:], in0=sigmas[:], in1=mid[:], op=ALU.subtract)
        nc.vector.tensor_copy(out=slopes[64:96, :], in_=sigmas[64:96, :])
        nc.vector.memset(slopes[96:128, :], 0.0)
        es = (
            [const.tile([P, 2, 12, 64], BF16, name="ea%d" % i) for i in range(N_E)],
            [const.tile([P, 2, 20, 64], BF16, name="eb%d" % i) for i in range(N_E)],
        )
        VARIANTS = {
            ("hi", 1): (0, 32, 128), ("hi", 2): (0, 64, 128), ("hi", 3): (0, 96, 128),
            ("lo", 0): (1, 0, 32), ("lo", 1): (1, 0, 64), ("lo", 2): (1, 0, 96),
            ("first", 2): (0, 0, 96), ("moved", 0): (0, 0, 32),
        }
        vvar = [
            {key: const.tile([P, GH * E], U32, name="v%s%d%d" % (key[0], key[1], i), align_bytes=64) for key in VARIANTS}
            for i in range(2)
        ]
        vmscales = [const.tile([P, GH * E], U8, name="vms%d" % i, align_bytes=64) for i in range(2)]

        zeros = const.tile([P, GH * E], U32, name="zeros")

        def zero_tiles():
            nc.vector.memset(zeros[:], 0)
            for scl in vmscales:
                nc.vector.memset(scl[:].bitcast(U32), 0)
            for e in es[0]:
                nc.vector.memset(e[:, :, 2:4, :], 0.0)

        def live(key):
            return (96, 128) if key[0] == "moved" else VARIANTS[key][1:]

        def zero_variants(i):
            for key in VARIANTS:
                for p0, p1 in ((0, live(key)[0]), (live(key)[1], P)):
                    if p0 < p1:
                        nc.sync.dma_start(
                            out=vvar[i][key][p0:p1, :].bitcast(I32), in_=zeros[p0:p1, :].bitcast(I32)
                        )

        def v_copy(hg, c, i):
            if i == 0:
                st["gv", hg, c] = vpool.tile([P, GH * E, 4], BF16, tag="gv", name="gv", align_bytes=64)
            cols = slice(i * E, (i + 1) * E)
            nc.gpsimd.tensor_scalar(
                out=st["gv", hg, c][:, cols, :],
                in0=st["vraw", hg][:, c, :, cols].rearrange("p t x -> p x t"),
                scalar1=1.0, scalar2=0.0, op0=ALU.mult, op1=ALU.add,
            )

        def v_quantise(hg, c):
            codes = vpool.tile([P, GH * E], U32, tag="vcodes%d" % c, name="vcodes", align_bytes=64)
            scl = vpool.tile([P, GH * E], U8, tag="vscales%d" % c, name="vscales", align_bytes=64)
            nc.vector.quantize_mx(
                out=codes[:].bitcast(FP8X4), scales=scl[:],
                in_=st["gv", hg, c][:].rearrange("p x t -> p (x t)"),
            )
            st["v", hg, c] = (codes, scl)
            for key, (half, p0, p1) in VARIANTS.items():
                if half == c:
                    q0, q1 = live(key)
                    nc.sync.dma_start(
                        out=vvar[hg % 2][key][q0:q1, :].bitcast(I32), in_=codes[p0:p1, :].bitcast(I32)
                    )
            if c == 0:
                nc.sync.dma_start(out=vmscales[hg % 2][96:100, :].bitcast(I32), in_=scl[0:4, :].bitcast(I32))

        Q_AT, K_AT = (0, 3 * GT), (GT, 2 * GT)

        def qk_transpose(h, half):
            x = st["x", h // GH]
            cols = slice((h % GH) * E, (h % GH + 1) * E)
            qk_ps = ps_a.tile([P, 2 * GT, P], BF16, tag="a", name="qk_ps")
            for w, at, order in ((0, Q_AT, ident_bf), (1, K_AT, perm_bf)):
                for j in range(GT):
                    nc.tensor.transpose(
                        qk_ps[:, at[half] - 2 * GT * half + j, :], x[:, w, GT * half + j, cols], order[:]
                    )
            st["qk_ps", h, half] = qk_ps

        def e_transpose(h, b):
            bank = ps_t.tile([P, 2, 2, P], F32, tag="tp", name="tp")
            for i, (half, s) in enumerate(SET_BANKS[b]):
                words = es[half][h % N_E][:].rearrange("p u s w -> p (u s w)").bitcast(F32)
                u_words = (20 if half else 12) * 32
                for u in range(2):
                    first = u * u_words + s * P
                    nc.tensor.transpose(bank[:, u, i, :], words[:, first : first + P], ident_f[:])
            st["bank", h, b] = bank

        def masks(h, bank):
            sb = ps_s.tile([P, 4 * P], F32, tag="s", name="sb")
            if bank == "window":
                blocks = range(4)
            else:
                blocks = {"q1": (1,), "q2q0": (2, 3)}.get(bank, (3,))
            for i, b in enumerate(blocks):
                nc.tensor.matmul(
                    sb[:, b * P : (b + 1) * P], lhsT=st["bias", h][:, int(bank == "window"), :], rhs=perm_f[:],
                    is_transpose=True, start=(i == 0), stop=False,
                )
            st["sb", h, bank] = sb

        def scores(h, bank):
            sb = st["sb", h, bank]
            qk_t = st["qk_t", h]

            def product(col, qb, k0, k1, stop):
                nc.tensor.matmul(
                    sb[:, col * P : (col + k1 - k0) * P], lhsT=qk_t[:, Q_AT[qb // GT] + qb % GT, :],
                    rhs=qk_t[:, K_AT[0] + k0 : K_AT[0] + k1, :], start=False, stop=stop,
                )

            def far(n):
                nc.tensor.matmul(
                    sb[:, 0 : n * P], lhsT=slopes[:, h : h + 1].to_broadcast([P, P]),
                    rhs=places[:, (3 - n) * P : 3 * P], start=False, stop=False,
                )

            if bank == "window":
                for j in range(GT):
                    product(j, GT + j, j, j + 1, j == GT - 1)
            elif bank == "q2q0":
                far(2)
                product(3, 0, 0, 1, False)
                product(0, 2, 0, 3, True)
            else:
                j = int(bank[1])
                qb = j + (GT if bank[0] == "m" else 0)
                k0 = max(0, qb - 3)
                far(qb - k0)
                product(0, qb, k0, qb + 1, True)

        def mx(h, half):
            hg = h // GH
            fcols = slice((h % GH) * E, (h % GH + 1) * E)
            (v0, s0), (v1, s1) = st["v", hg, 0], st["v", hg, 1]
            var = vvar[hg % 2]
            if half == 0:
                passes = [
                    [(1, var["moved", 0], vmscales[hg % 2])],
                    [(0, v0, s0)],
                    [(1, var["first", 2], s0)],
                    [(2, v0, s0)],
                ]
            else:
                passes = [
                    [(j, var["hi", j] if j else v0, s0), (j + 1, var["lo", j] if j < 3 else v1, s1)]
                    for j in range(GT)
                ]
            ob = ps_a.tile([P, GT, P], F32, tag="a", name="ob")
            for j in range(GT):
                for i, (s, vc, vs) in enumerate(passes[j]):
                    codes, scl, qcols = st["codes", h, half, s]
                    nc.tensor.matmul_mx(
                        out=ob[:, j, :],
                        lhsT=codes[:, qcols].bitcast(FP8X4),
                        lhsT_scale=scl[:, qcols],
                        rhs=vc[:, fcols].bitcast(FP8X4),
                        rhs_scale=vs[:, fcols],
                        start=(i == 0),
                        stop=(i == len(passes[j]) - 1),
                    )
            st["ob", h, half] = ob

        def score_pass(h, bank):
            sb = st["sb", h, bank]

            def one(z_out, col, n, first, least):
                nc.vector.tensor_scalar(
                    out=z_out, in0=sb[:, col * P : (col + n) * P], scalar1=-SCALE, scalar2=first,
                    op0=ALU.mult, op1=ALU.min, accum_out=least,
                )

            if bank == "window":
                mw = gsmall.tile([P, GT], F32, tag="mw", name="mw")
                for j in range(GT):
                    z = zpool.tile([P, 5 * P], F32, tag="zm", name="z")
                    one(z[:, 0:P], j, 1, None, mw[:, j : j + 1])
                    st["z", h, "m%d" % j] = z
                    st["first", h, "m%d" % j] = mw[:, j : j + 1]
                return
            parts = {"q1": (("q1", 0, 2),), "q2q0": (("q2", 0, 3), ("q0", 3, 1))}.get(bank, ((bank, 0, 4),))
            for tile, col, n in parts:
                nbias = small.tile([P, 1], F32, tag="nbias", name="nbias")
                if tile[0] == "m":
                    one(st["z", h, tile][:, P : 5 * P], col, n, st["first", h, tile], nbias[:])
                else:
                    z = zpool.tile([P, 4 * P], F32, tag="zq", name="z")
                    one(z[:, 0 : n * P], col, n, None, nbias[:])
                    st["z", h, tile] = z
                st["nbias", h, tile] = nbias

        def quantise(h, b):
            if h == H - 1:
                first, banks = 2 * (b % 2), SET_BANKS[b]
            elif b % 2 == 0:
                return
            else:
                first, banks = 0, SET_BANKS[b - 1] + SET_BANKS[b]
            n = len(banks)
            codes = cpool.tile([P, 4 * P], U32, tag="codes", name="codes", align_bytes=64)
            scl = cpool.tile([P, 4 * P], U8, tag="scl", name="scl", align_bytes=64)
            nc.vector.quantize_mx(
                out=codes[:, 0 : n * P].bitcast(FP8X4), scales=scl[:, 0 : n * P],
                in_=st["grp", h, b // 2][:, first : first + n].rearrange("p g q t -> p (g q t)"),
            )
            for i, (half, s) in enumerate(banks):
                st["codes", h, half, s] = (codes, scl, slice(i * P, (i + 1) * P))

        def reciprocals(h):
            st["rinv", h] = gsmall.tile([P, 2, GT], F32, tag="rinv", name="rinv")
            nc.vector.reciprocal(out=st["rinv", h][:], in_=st["rs", h][:])

        def store(h, half):
            rinv = st["rinv", h][:, half, :]
            ost = opool.tile([P, GT, P], F32, tag="ost", name="ost")
            nc.vector.tensor_tensor(
                out=ost[:], in0=st["ob", h, half][:], in1=rinv.unsqueeze(2).to_broadcast([P, GT, P]),
                op=ALU.mult,
            )
            nc.sync.dma_start(
                out=out[0, 512 * half : 512 * half + 512, h, :].rearrange("(b p) e -> p b e", p=P), in_=ost[:]
            )

        def exp(h, tile):
            half, j = int(tile[0] == "m"), int(tile[1])
            if ("rs", h) not in st:
                st["rs", h] = gsmall.tile([P, 2, GT], F32, tag="rs", name="rs")
            n = 5 if half else j + 1
            nc.scalar.activation(
                out=es[half][h % N_E][:, :, SLOTS[tile] : SLOTS[tile] + n, :],
                in_=st["z", h, tile][:, 0 : n * P].rearrange("p (b u w) -> p u b w", u=2, w=64),
                func=ACT.Exp, bias=st["nbias", h, tile][:], scale=-1.0,
                accum_out=st["rs", h][:, half, j : j + 1],
            )

        def e_copy(h, b):
            if b % 2 == 0:
                st["grp", h, b // 2] = gpool.tile([P, 4, P, 4], BF16, tag="grp", name="grp", align_bytes=64)
            grp = st["grp", h, b // 2]
            words = grp[:].rearrange("p c q t -> p (c q t)").bitcast(F32).rearrange("p (c q u) -> p c q u", c=4, u=2)
            i = 2 * (b % 2)
            nc.scalar.copy(out=words[:, i : i + 2], in_=st["bank", h, b][:].rearrange("p u c q -> p c q u"))

        def qk_copy(h, half):
            if half == 0:
                st["qk_t", h] = kpool.tile([P, 4 * GT, P], BF16, tag="qk_t", name="qk_t")
            nc.scalar.copy(
                out=st["qk_t", h][:, 2 * GT * half : 2 * GT * (half + 1), :].bitcast(F32),
                in_=st["qk_ps", h, half][:].bitcast(F32),
            )

        def score_banks(k):
            h, p = divmod(k, 4)
            return [(h + dh, bank) for bank, dh in SCORE_BANKS[p] if 0 <= h + dh < H and 0 <= h + 1]

        def head_at(k, at):
            h, r = divmod(k - at, 4)
            return h if r == 0 and 0 <= h < H else None

        def set_bank_at(k):
            h, b = divmod(k - AT_TR, 4)
            return (h, b) if 0 <= h < H else None

        def mx_at(k):
            for half in (1, 0):
                h = head_at(k, AT_MX[half])
                if h is not None:
                    mx(h, half)

        v_plan = {}
        for hg in range(NHG):
            for c in range(2):
                base, (at_copy, at_q) = (0, V_FIRST[c]) if hg == 0 else (16 * (hg - 1), V_NEXT[c])
                for i in range(4):
                    v_plan.setdefault(base + at_copy[i], []).append((v_copy, hg, c, i))
                v_plan.setdefault(base + at_q, []).append((v_quantise, hg, c))

        for k in range(AT_BIAS, 4 * H + AT_MX[0] + 2):
            if set_bank_at(k):
                e_transpose(*set_bank_at(k))
            qk_at_k = [(h, half) for half in range(2) for h in (head_at(k, AT_QKT[half]),) if h is not None]
            for h, bank in score_banks(k):
                masks(h, bank)
            for i, (h, bank) in enumerate(score_banks(k)):
                if i == 1:
                    mx_at(k)
                    if k > 0:
                        for hq, half in qk_at_k:
                            qk_transpose(hq, half)
                scores(h, bank)
            if len(score_banks(k)) < 2:
                mx_at(k)
            if k <= 0:
                for h, half in qk_at_k:
                    qk_transpose(h, half)
            h = head_at(k, AT_BIAS)
            if h:
                h_bias(h)
            for h, bank in score_banks(k - LAG_PASS):
                score_pass(h, bank)
            if set_bank_at(k - LAG_Q):
                quantise(*set_bank_at(k - LAG_Q))
            h = head_at(k, AT_RINV)
            if h is not None:
                reciprocals(h)
            if k == 2:
                zero_tiles()
                zero_variants(0)
            if k == 6:
                zero_variants(1)
            for half in (1, 0):
                h = head_at(k, AT_MX[half] + 1)
                if h is not None:
                    store(h, half)
            for stage, *index in v_plan.get(k, []):
                stage(*index)
            if 0 <= k - LAG_EXP < 4 * H:
                for tile in EXPS[(k - LAG_EXP) % 4]:
                    exp((k - LAG_EXP) // 4, tile)
            if set_bank_at(k):
                e_copy(*set_bank_at(k))
            for h, half in qk_at_k:
                qk_copy(h, half)
            hg, r = divmod(k + 22, 16)
            if 2 <= hg < NHG and r < 2:
                load_qk(hg, r)
                load_v(hg, r)
